import numpy as np
import ml_dtypes


def mxq(x, axis, fmt="e4m3"):
    dtype, down = {"e4m3": (ml_dtypes.float8_e4m3fn, 7), "e5m2": (ml_dtypes.float8_e5m2, 14)}[fmt]
    v = np.moveaxis(np.asarray(x, np.float32).astype(ml_dtypes.bfloat16).astype(np.float64), axis, -1)
    blocks = v.reshape(v.shape[:-1] + (-1, 32))
    amax = np.abs(blocks).max(-1, keepdims=True)
    byte = np.maximum(np.where(amax > 0, np.frexp(amax)[1] - 1 + 127, 0) - down, 1)
    scale = np.exp2(byte - 127.0)
    codes = (blocks / scale).astype(np.float32).astype(dtype).astype(np.float64)
    return np.moveaxis((codes * scale).reshape(v.shape), -1, axis)


WIDE = False


def mx_kscale(k):
    if not WIDE:
        return np.ones(k)
    levels = np.array([10, -10, 5, -5, 0])
    a = np.random.permutation(np.resize(levels, k // 512 * 4)).reshape(k // 512, 4)
    idx = np.arange(k)
    return np.exp2(a[idx // 512, idx % 128 // 32])


BF16 = ml_dtypes.bfloat16


def bf(x):
    return np.asarray(x, np.float32).astype(BF16)


def f64(x):
    return np.asarray(x).astype(np.float64)


B, I, H = 1024, 512, 1024
SPARSITY = 0.5
TS = 1.0


def erf(v):
    a = np.minimum(np.abs(v), 6.0)
    q = 2.0 * a * a
    term, total, n = a, a, 0
    while np.any(term > 1e-18 * total):
        n += 1
        term = term * (q / (2 * n + 1))
        total = total + term
    return np.sign(v) * total * np.exp(-a * a) * 2.0 / np.sqrt(np.pi)


def gelu(v):
    return 0.5 * v * (1.0 + erf(v / np.sqrt(2.0)))


def sigmoid(v):
    return 1.0 / (1.0 + np.exp(-v))


def setup_inputs():
    s, u = mx_kscale(H), mx_kscale(I)
    rn = np.random.standard_normal
    keep = np.random.random((H, H)) > SPARSITY
    return {"ff1": bf(gelu(rn((B, H))) * s), "x": bf(rn((B, I)) * u), "hx": bf(rn((B, H))),
            "W_ff2": bf(rn((H, H)) * 1.5 / np.sqrt(H) / s), "b_ff2": bf(rn(H) * 0.3),
            "W_ta": bf(rn((H, H)) * 1.5 / np.sqrt(H)), "b_ta": bf(rn(H) * 0.3),
            "W_tb": bf(rn((H, H)) * 1.5 / np.sqrt(H)), "b_tb": bf(rn(H) * 0.3),
            "W_in": bf(rn((H, I)) / np.sqrt(I) / u), "b_in": bf(rn(H) * 0.3), "input_b": bf(rn(H) * 0.3),
            "W_r": bf(rn((H, H)) * keep / np.sqrt((1.0 - SPARSITY) * H)), "r_b": bf(rn(H) * 0.3)}


def reference(ff1, x, hx, W_ff2, b_ff2, W_ta, b_ta, W_tb, b_tb, W_in, b_in, input_b, W_r, r_b):
    h0 = f64(hx)
    ff2 = gelu((mxq(f64(ff1), 1, "e4m3") @ mxq(f64(W_ff2), 1, "e4m3").T) + f64(b_ff2))
    ff2q = mxq(ff2, 1, "e4m3")
    t_a = (ff2q @ mxq(f64(W_ta), 1, "e4m3").T) + f64(b_ta)
    t_b = (ff2q @ mxq(f64(W_tb), 1, "e4m3").T) + f64(b_tb)
    t_interp = sigmoid(t_a * TS + t_b)
    input_contrib = gelu((mxq(f64(x), 1, "e4m3") @ mxq(f64(W_in), 1, "e4m3").T) + f64(b_in) + f64(input_b))
    recurrent_contrib = gelu((mxq(h0, 1, "e4m3") @ mxq(f64(W_r), 1, "e4m3").T) + f64(r_b))
    return h0 * (1.0 - t_interp) + t_interp * (input_contrib + recurrent_contrib)

@@ -1,0 +1,282 @@
+from contextlib import ExitStack
+
+import concourse.mybir as mybir
+from concourse.masks import make_identity
+
+F32 = mybir.dt.float32
+BF16 = mybir.dt.bfloat16
+U32 = mybir.dt.uint32
+U8 = mybir.dt.uint8
+FP8X4 = mybir.dt.float8_e4m3fn_x4
+ACT = mybir.ActivationFunctionType
+ALU = mybir.AluOpType
+
+P = 128
+BATCH, IN_FEATURES, HIDDEN = 1024, 512, 1024
+FLOPS = 2 * BATCH * HIDDEN * (4 * HIDDEN + IN_FEATURES)
+
+K_PASS = 512
+WORDS = K_PASS // 2
+CHUNK = 512
+CHUNKS = BATCH // CHUNK
+ROWS = BATCH // P
+CHUNK_ROWS = CHUNK // P
+PAIRS = HIDDEN // (2 * P)
+TILES = 2 * PAIRS
+UNIT = 2048
+UNIT_COLS = UNIT // 4
+
+HEAD = 5
+PER_STEP = 2
+
+
+def tile_cfccell_pa_kernel(
+    tc, ff1, x, hx, W_ff2, b_ff2, W_ta, b_ta, W_tb, b_tb, W_in, b_in, input_b, W_r, r_b, out
+):
+    nc = tc.nc
+    with ExitStack() as ctx:
+        keep = ctx.enter_context(tc.tile_pool(name="keep", bufs=1))
+        stream = ctx.enter_context(tc.tile_pool(name="stream", bufs=8))
+        stage = ctx.enter_context(tc.tile_pool(name="stage", bufs=4))
+        work = ctx.enter_context(tc.tile_pool(name="work", bufs=3))
+        psum_t = ctx.enter_context(tc.psum_pool(name="psum_t", bufs=4))
+        psum_z = ctx.enter_context(tc.psum_pool(name="psum_z", bufs=4))
+
+        ident = keep.tile([P, P], F32, name="ident")
+        make_identity(nc, ident[:])
+
+        warm = keep.tile([P, 1], F32, name="warm")
+        nc.vector.memset(warm[:], 0.0)
+        nc.scalar.activation(out=warm[:], in_=warm[:], func=ACT.Gelu)
+
+        bias_rows = keep.tile([P, 2 * P], BF16, name="bias_rows")
+        nc.vector.memset(bias_rows[:], 0.0)
+        for v, vector in enumerate((b_ff2, b_ta, b_tb, b_in, input_b, r_b)):
+            nc.scalar.dma_start(
+                out=bias_rows[PAIRS * v : PAIRS * (v + 1), :],
+                in_=vector.rearrange("(a w) -> a w", a=PAIRS),
+            )
+
+        def mx_operand(name, columns):
+            codes = keep.tile([P, columns], U32, name=name + "_codes", align_bytes=64)
+            scales = keep.tile([P, columns], U8, name=name + "_scales", align_bytes=64)
+            return codes, scales
+
+        def columns(operand, first, count):
+            codes, scales = operand
+            return codes[:, first : first + count], scales[:, first : first + count]
+
+        ff1_q = mx_operand("ff1", 2 * BATCH)
+        hx_q = mx_operand("hx", 2 * BATCH)
+        ff2_q = mx_operand("ff2", 2 * BATCH)
+        x_q = mx_operand("x", BATCH)
+        wff2_q = mx_operand("wff2", 2 * HIDDEN)
+        wta_q = mx_operand("wta", 2 * HIDDEN)
+        wtb_q = mx_operand("wtb", 2 * HIDDEN)
+        wr_q = mx_operand("wr", 2 * HIDDEN)
+        win_q = mx_operand("win", HIDDEN)
+
+        def moving(operand, c, g):
+            return columns(operand, BATCH * g + CHUNK * c, CHUNK)
+
+        def stationary(operand, a, e, g):
+            return columns(operand, UNIT_COLS * a + P * (2 * e + g), P)
+
+        def mx_pass(acc, weights, acts, start, stop):
+            nc.tensor.matmul_mx(
+                out=acc[:],
+                lhsT=weights[0].bitcast(FP8X4),
+                lhsT_scale=weights[1],
+                rhs=acts[0].bitcast(FP8X4),
+                rhs_scale=acts[1],
+                start=start,
+                stop=stop,
+            )
+
+        def pack(blocks, grouped, copy_out, dest):
+            words = grouped[:].bitcast(F32).rearrange("p (b r u) -> p b r u", b=4, u=2)
+            for half in range(2):
+                bank = psum_t.tile([P, 2, 2, P], F32, name="bank")
+                for b in range(2):
+                    for u in range(2):
+                        nc.tensor.transpose(bank[:, b, u, :], blocks[:, 2 * half + b, u, :], ident[:])
+                copy_out(
+                    out=words[:, 2 * half : 2 * half + 2, :, :],
+                    in_=bank[:].rearrange("p b u r -> p b r u"),
+                )
+            codes, scales = dest
+            nc.vector.quantize_mx(out=codes.bitcast(FP8X4), scales=scales, in_=grouped[:])
+
+        def prepare_streamed(pieces, dest):
+            raw = stream.tile([P, UNIT], BF16, name="raw")
+            landing = raw[:].rearrange("p (b k) -> p b k", b=4)
+            first = 0
+            for piece in pieces:
+                nc.sync.dma_start(out=landing[:, first : first + piece.shape[1], :], in_=piece)
+                first += piece.shape[1]
+            grouped = stage.tile([P, UNIT], BF16, name="grouped", align_bytes=64)
+            blocks = raw[:].bitcast(F32).rearrange("p (b u w) -> p b u w", b=4, u=2)
+            pack(blocks, grouped, nc.scalar.copy, dest)
+
+        hx_nat = keep.tile([P, ROWS * HIDDEN], BF16, name="hx_nat")
+        hx_rows = hx_nat[:].rearrange("p (n k) -> p n k", n=ROWS)
+        hx_words = hx_nat[:].bitcast(F32).rearrange("p (n w) -> p n w", n=ROWS)
+        hx_dram = hx.rearrange("(p n) k -> p n k", n=ROWS)
+        hx_grouped = {}
+        for c in range(CHUNKS):
+            for g in range(2):
+                hx_grouped[c, g] = keep.tile(
+                    [P, UNIT], BF16, name="hx_grouped_%d_%d" % (c, g), align_bytes=64
+                )
+
+        def prepare_state(c, g):
+            rows = slice(CHUNK_ROWS * c, CHUNK_ROWS * (c + 1))
+            ks = slice(K_PASS * g, K_PASS * (g + 1))
+            nc.sync.dma_start(out=hx_rows[:, rows, ks], in_=hx_dram[:, rows, ks])
+            blocks = hx_words[:, rows, WORDS * g : WORDS * (g + 1)].rearrange(
+                "p n (u w) -> p n u w", u=2
+            )
+            pack(blocks, hx_grouped[c, g], nc.vector.tensor_copy, moving(hx_q, c, g))
+
+        def activation_unit(source, operand, c, g):
+            rows = source.rearrange("(p n) k -> p n k", n=ROWS)[
+                :, CHUNK_ROWS * c : CHUNK_ROWS * (c + 1), K_PASS * g : K_PASS * (g + 1)
+            ]
+            return prepare_streamed, ([rows], moving(operand, c, g))
+
+        def weight_unit(source, operand, a):
+            rows = source.rearrange("(a p e) k -> a p (e k)", p=P, e=2)[a]
+            blocks = rows.rearrange("p (b k) -> p b k", b=4)
+            return prepare_streamed, ([blocks], columns(operand, UNIT_COLS * a, UNIT_COLS))
+
+        def input_weight_unit(h):
+            rows = W_in.rearrange("(a p e) k -> a p e k", p=P, e=2)
+            return prepare_streamed, ([rows[2 * h], rows[2 * h + 1]], columns(win_q, UNIT_COLS * h, UNIT_COLS))
+
+        units = [activation_unit(ff1, ff1_q, 0, g) for g in range(2)]
+        units += [weight_unit(W_ff2, wff2_q, a) for a in range(PAIRS)]
+        units += [activation_unit(ff1, ff1_q, 1, g) for g in range(2)]
+        units += [activation_unit(x, x_q, c, 0) for c in range(CHUNKS)]
+        units += [(prepare_state, (c, g)) for c in range(CHUNKS) for g in range(2)]
+        for a in range(PAIRS):
+            if a % 2 == 0:
+                units.append(input_weight_unit(a // 2))
+            units += [weight_unit(W_r, wr_q, a), weight_unit(W_ta, wta_q, a), weight_unit(W_tb, wtb_q, a)]
+
+        def prepare_units(first, count):
+            for prepare, args in units[first : first + count]:
+                prepare(*args)
+
+        ff2_rows = {}
+
+        def first_layer_pair(c, a):
+            g2, u = divmod(a, 2)
+            if u == 0:
+                ff2_rows[c, g2] = work.tile([P, 4, CHUNK], BF16, name="ff2_rows", bufs=2)
+            for e in range(2):
+                acc = psum_z.tile([P, CHUNK], F32, name="acc")
+                for g in range(2):
+                    mx_pass(acc, stationary(wff2_q, a, e, g), moving(ff1_q, c, g), g == 0, g == 1)
+                nc.scalar.activation(
+                    out=ff2_rows[c, g2][:, 2 * u + e, :],
+                    in_=acc[:],
+                    func=ACT.Gelu,
+                    bias=bias[:, 0, 2 * a + e : 2 * a + e + 1],
+                )
+            if u == 1:
+                grouped = stage.tile([P, UNIT], BF16, name="grouped", align_bytes=64)
+                nc.vector.tensor_copy(
+                    out=grouped[:].rearrange("p (r t) -> p r t", t=4),
+                    in_=ff2_rows[c, g2][:].rearrange("p t r -> p r t"),
+                )
+                codes, scales = moving(ff2_q, c, g2)
+                nc.vector.quantize_mx(out=codes.bitcast(FP8X4), scales=scales, in_=grouped[:])
+
+        def blend_pair(c, a):
+            blend = work.tile([P, 2, CHUNK], F32, name="blend")
+            g_hx, u_hx = divmod(a, 2)
+            hx_t = hx_grouped[c, g_hx][:].rearrange("p (r t) -> p r t", t=4)
+            for e in range(2):
+                j = 2 * a + e
+                acc_in = psum_z.tile([P, CHUNK], F32, name="acc")
+                mx_pass(acc_in, columns(win_q, P * j, P), moving(x_q, c, 0), True, True)
+                cand = work.tile([P, CHUNK], F32, name="cand")
+                nc.scalar.activation(out=cand[:], in_=acc_in[:], func=ACT.Gelu, bias=bias_cand[:, j : j + 1])
+
+                acc_rec = psum_z.tile([P, CHUNK], F32, name="acc")
+                for g in range(2):
+                    mx_pass(acc_rec, stationary(wr_q, a, e, g), moving(hx_q, c, g), g == 0, g == 1)
+                rec = work.tile([P, CHUNK], F32, name="rec")
+                nc.scalar.activation(out=rec[:], in_=acc_rec[:], func=ACT.Gelu, bias=bias[:, 5, j : j + 1])
+
+                acc_gate = psum_z.tile([P, CHUNK], F32, name="acc")
+                for i, w_q in enumerate((wta_q, wtb_q)):
+                    for g in range(2):
+                        mx_pass(acc_gate, stationary(w_q, a, e, g), moving(ff2_q, c, g), i + g == 0, i + g == 2)
+                gate = work.tile([P, CHUNK], F32, name="gate")
+                nc.scalar.activation(
+                    out=gate[:], in_=acc_gate[:], func=ACT.Tanh, bias=bias_gate[:, j : j + 1], scale=0.5
+                )
+
+                nc.vector.tensor_tensor(out=cand[:], in0=cand[:], in1=rec[:], op=ALU.add)
+                nc.vector.tensor_tensor(out=cand[:], in0=cand[:], in1=hx_t[:, :, 2 * u_hx + e], op=ALU.subtract)
+                nc.vector.scalar_tensor_tensor(
+                    out=blend[:, e, :], in0=gate[:], scalar=1.0, in1=cand[:], op0=ALU.add, op1=ALU.mult
+                )
+            return blend
+
+        out_dram = out.rearrange("(p n) h -> p n h", n=ROWS)
+
+        def finish(c, a, blend, queue):
+            out_rows = work.tile([P, CHUNK_ROWS, 2 * P], F32, name="out_rows")
+            features = slice(2 * P * a, 2 * P * (a + 1))
+            for half in range(2):
+                bank = psum_t.tile([P, 2, 2, P], F32, name="bank")
+                for e in range(2):
+                    for n in range(2):
+                        r = P * (2 * half + n)
+                        nc.tensor.transpose(bank[:, e, n, :], blend[:, e, r : r + P], ident[:])
+                first = CHUNK_ROWS * c + 2 * half
+                nc.vector.scalar_tensor_tensor(
+                    out=out_rows[:, 2 * half : 2 * half + 2, :].rearrange("b n (p e) -> b n p e", e=2),
+                    in0=bank[:].rearrange("b e n p -> b n p e"),
+                    scalar=0.5,
+                    in1=hx_rows[:, first : first + 2, features].rearrange("b n (p e) -> b n p e", e=2),
+                    op0=ALU.mult,
+                    op1=ALU.add,
+                )
+            queue.dma_start(
+                out=out_dram[:, CHUNK_ROWS * c : CHUNK_ROWS * (c + 1), features], in_=out_rows[:]
+            )
+
+        prepare_units(0, HEAD)
+
+        bank = psum_t.tile([P, 2, 2, P], F32, name="bank")
+        nc.tensor.transpose(bank[:, 0, 0, :], bias_rows[:].bitcast(F32), ident[:])
+        bias_pairs = keep.tile([P, 2 * P], BF16, name="bias_pairs")
+        nc.vector.tensor_copy(out=bias_pairs[:].bitcast(F32), in_=bank[:, 0, 0, :])
+        bias = keep.tile([P, 6, TILES], F32, name="bias")
+        nc.vector.tensor_copy(out=bias[:].rearrange("p v j -> p (v j)"), in_=bias_pairs[:, 0 : 6 * TILES])
+        bias_gate = keep.tile([P, TILES], F32, name="bias_gate")
+        nc.vector.tensor_tensor(out=bias_gate[:], in0=bias[:, 1, :], in1=bias[:, 2, :], op=ALU.add)
+        nc.vector.tensor_scalar_mul(out=bias_gate[:], in0=bias_gate[:], scalar1=0.5)
+        bias_cand = keep.tile([P, TILES], F32, name="bias_cand")
+        nc.vector.tensor_tensor(out=bias_cand[:], in0=bias[:, 3, :], in1=bias[:, 4, :], op=ALU.add)
+
+        step = 0
+        for c in range(CHUNKS):
+            for a in range(PAIRS):
+                first_layer_pair(c, a)
+                prepare_units(HEAD + PER_STEP * step, PER_STEP)
+                step += 1
+        waiting = None
+        for a in range(PAIRS):
+            for c in range(CHUNKS):
+                blend = blend_pair(c, a)
+                prepare_units(HEAD + PER_STEP * step, PER_STEP)
+                step += 1
+                if waiting is not None:
+                    finish(*waiting)
+                loads_left = HEAD + PER_STEP * (step + 1) < len(units)
+                waiting = (c, a, blend, nc.gpsimd if loads_left else nc.sync)
+        finish(*waiting)

@@ -26,7 +26,7 @@ TILES = 2 * PAIRS
 UNIT = 2048
 UNIT_COLS = UNIT // 4
 
-HEAD = 5
+HEAD = 4
 PER_STEP = 2
 
 
@@ -37,10 +37,11 @@ def tile_cfccell_pa_kernel(
     with ExitStack() as ctx:
         keep = ctx.enter_context(tc.tile_pool(name="keep", bufs=1))
         stream = ctx.enter_context(tc.tile_pool(name="stream", bufs=8))
-        stage = ctx.enter_context(tc.tile_pool(name="stage", bufs=4))
+        stage = ctx.enter_context(tc.tile_pool(name="stage", bufs=5))
         work = ctx.enter_context(tc.tile_pool(name="work", bufs=3))
-        psum_t = ctx.enter_context(tc.psum_pool(name="psum_t", bufs=4))
-        psum_z = ctx.enter_context(tc.psum_pool(name="psum_z", bufs=4))
+        psum_t = ctx.enter_context(tc.psum_pool(name="psum_t", bufs=5))
+        psum_z = ctx.enter_context(tc.psum_pool(name="psum_z", bufs=3))
+        ctx.enter_context(tc.manual_schedule())
 
         ident = keep.tile([P, P], F32, name="ident")
         make_identity(nc, ident[:])
@@ -57,9 +58,9 @@ def tile_cfccell_pa_kernel(
                 in_=vector.rearrange("(a w) -> a w", a=PAIRS),
             )
 
-        def mx_operand(name, columns):
-            codes = keep.tile([P, columns], U32, name=name + "_codes", align_bytes=64)
-            scales = keep.tile([P, columns], U8, name=name + "_scales", align_bytes=64)
+        def mx_operand(name, width):
+            codes = keep.tile([P, width], U32, name=name + "_codes", align_bytes=64)
+            scales = keep.tile([P, width], U8, name=name + "_scales", align_bytes=64)
             return codes, scales
 
         def columns(operand, first, count):
@@ -93,21 +94,24 @@ def tile_cfccell_pa_kernel(
                 stop=stop,
             )
 
-        def pack(blocks, grouped, copy_out, dest):
+        def transpose_unit(blocks, grouped, vector_helps):
             words = grouped[:].bitcast(F32).rearrange("p (b r u) -> p b r u", b=4, u=2)
             for half in range(2):
                 bank = psum_t.tile([P, 2, 2, P], F32, name="bank")
                 for b in range(2):
                     for u in range(2):
                         nc.tensor.transpose(bank[:, b, u, :], blocks[:, 2 * half + b, u, :], ident[:])
+                copy_out = nc.vector.tensor_copy if vector_helps and half == 1 else nc.scalar.copy
                 copy_out(
                     out=words[:, 2 * half : 2 * half + 2, :, :],
                     in_=bank[:].rearrange("p b u r -> p b r u"),
                 )
-            codes, scales = dest
-            nc.vector.quantize_mx(out=codes.bitcast(FP8X4), scales=scales, in_=grouped[:])
 
-        def prepare_streamed(pieces, dest):
+        def quantise(ready):
+            for grouped, (codes, scales) in ready:
+                nc.vector.quantize_mx(out=codes.bitcast(FP8X4), scales=scales, in_=grouped[:])
+
+        def prepare_streamed(pieces, dest, vector_helps):
             raw = stream.tile([P, UNIT], BF16, name="raw")
             landing = raw[:].rearrange("p (b k) -> p b k", b=4)
             first = 0
@@ -116,7 +120,8 @@ def tile_cfccell_pa_kernel(
                 first += piece.shape[1]
             grouped = stage.tile([P, UNIT], BF16, name="grouped", align_bytes=64)
             blocks = raw[:].bitcast(F32).rearrange("p (b u w) -> p b u w", b=4, u=2)
-            pack(blocks, grouped, nc.scalar.copy, dest)
+            transpose_unit(blocks, grouped, vector_helps)
+            return grouped, dest
 
         hx_nat = keep.tile([P, ROWS * HIDDEN], BF16, name="hx_nat")
         hx_rows = hx_nat[:].rearrange("p (n k) -> p n k", n=ROWS)
@@ -129,14 +134,15 @@ def tile_cfccell_pa_kernel(
                     [P, UNIT], BF16, name="hx_grouped_%d_%d" % (c, g), align_bytes=64
                 )
 
-        def prepare_state(c, g):
+        def prepare_state(c, g, vector_helps):
             rows = slice(CHUNK_ROWS * c, CHUNK_ROWS * (c + 1))
             ks = slice(K_PASS * g, K_PASS * (g + 1))
             nc.sync.dma_start(out=hx_rows[:, rows, ks], in_=hx_dram[:, rows, ks])
             blocks = hx_words[:, rows, WORDS * g : WORDS * (g + 1)].rearrange(
                 "p n (u w) -> p n u w", u=2
             )
-            pack(blocks, hx_grouped[c, g], nc.vector.tensor_copy, moving(hx_q, c, g))
+            transpose_unit(blocks, hx_grouped[c, g], vector_helps)
+            return hx_grouped[c, g], moving(hx_q, c, g)
 
         def activation_unit(source, operand, c, g):
             rows = source.rearrange("(p n) k -> p n k", n=ROWS)[
@@ -163,9 +169,11 @@ def tile_cfccell_pa_kernel(
                 units.append(input_weight_unit(a // 2))
             units += [weight_unit(W_r, wr_q, a), weight_unit(W_ta, wta_q, a), weight_unit(W_tb, wtb_q, a)]
 
-        def prepare_units(first, count):
-            for prepare, args in units[first : first + count]:
-                prepare(*args)
+        def prepare_units(first, count, vector_helps):
+            return [
+                prepare(*args, vector_helps and i % 2 == 1)
+                for i, (prepare, args) in enumerate(units[first : first + count])
+            ]
 
         ff2_rows = {}
 
@@ -183,52 +191,57 @@ def tile_cfccell_pa_kernel(
                     func=ACT.Gelu,
                     bias=bias[:, 0, 2 * a + e : 2 * a + e + 1],
                 )
-            if u == 1:
-                grouped = stage.tile([P, UNIT], BF16, name="grouped", align_bytes=64)
-                nc.vector.tensor_copy(
-                    out=grouped[:].rearrange("p (r t) -> p r t", t=4),
-                    in_=ff2_rows[c, g2][:].rearrange("p t r -> p r t"),
-                )
-                codes, scales = moving(ff2_q, c, g2)
-                nc.vector.quantize_mx(out=codes.bitcast(FP8X4), scales=scales, in_=grouped[:])
+            if u == 0:
+                return []
+            grouped = stage.tile([P, UNIT], BF16, name="grouped", align_bytes=64)
+            nc.vector.tensor_copy(
+                out=grouped[:].rearrange("p (r t) -> p r t", t=4),
+                in_=ff2_rows[c, g2][:].rearrange("p t r -> p r t"),
+            )
+            return [(grouped, moving(ff2_q, c, g2))]
 
         def blend_pair(c, a):
-            blend = work.tile([P, 2, CHUNK], F32, name="blend")
+            tiles = range(2)
+            cand = work.tile([P, 2, CHUNK], F32, name="cand")
+            for e in tiles:
+                acc = psum_z.tile([P, CHUNK], F32, name="acc")
+                mx_pass(acc, columns(win_q, P * (2 * a + e), P), moving(x_q, c, 0), True, True)
+                nc.scalar.activation(
+                    out=cand[:, e, :], in_=acc[:], func=ACT.Gelu, bias=bias_cand[:, 2 * a + e : 2 * a + e + 1]
+                )
             g_hx, u_hx = divmod(a, 2)
-            hx_t = hx_grouped[c, g_hx][:].rearrange("p (r t) -> p r t", t=4)
-            for e in range(2):
-                j = 2 * a + e
-                acc_in = psum_z.tile([P, CHUNK], F32, name="acc")
-                mx_pass(acc_in, columns(win_q, P * j, P), moving(x_q, c, 0), True, True)
-                cand = work.tile([P, CHUNK], F32, name="cand")
-                nc.scalar.activation(out=cand[:], in_=acc_in[:], func=ACT.Gelu, bias=bias_cand[:, j : j + 1])
-
-                acc_rec = psum_z.tile([P, CHUNK], F32, name="acc")
+            hx_t = hx_grouped[c, g_hx][:].rearrange("p (r t) -> p t r", t=4)
+            nc.vector.tensor_tensor(
+                out=cand[:], in0=cand[:], in1=hx_t[:, 2 * u_hx : 2 * u_hx + 2, :], op=ALU.subtract
+            )
+            for e in tiles:
+                acc = psum_z.tile([P, CHUNK], F32, name="acc")
                 for g in range(2):
-                    mx_pass(acc_rec, stationary(wr_q, a, e, g), moving(hx_q, c, g), g == 0, g == 1)
+                    mx_pass(acc, stationary(wr_q, a, e, g), moving(hx_q, c, g), g == 0, g == 1)
                 rec = work.tile([P, CHUNK], F32, name="rec")
-                nc.scalar.activation(out=rec[:], in_=acc_rec[:], func=ACT.Gelu, bias=bias[:, 5, j : j + 1])
-
-                acc_gate = psum_z.tile([P, CHUNK], F32, name="acc")
+                nc.scalar.activation(
+                    out=rec[:], in_=acc[:], func=ACT.Gelu, bias=bias[:, 5, 2 * a + e : 2 * a + e + 1]
+                )
+                nc.vector.tensor_tensor(out=cand[:, e, :], in0=cand[:, e, :], in1=rec[:], op=ALU.add)
+            blend = work.tile([P, 2, CHUNK], F32, name="blend")
+            for e in tiles:
+                acc = psum_z.tile([P, CHUNK], F32, name="acc")
                 for i, w_q in enumerate((wta_q, wtb_q)):
                     for g in range(2):
-                        mx_pass(acc_gate, stationary(w_q, a, e, g), moving(ff2_q, c, g), i + g == 0, i + g == 2)
+                        mx_pass(acc, stationary(w_q, a, e, g), moving(ff2_q, c, g), i + g == 0, i + g == 2)
                 gate = work.tile([P, CHUNK], F32, name="gate")
                 nc.scalar.activation(
-                    out=gate[:], in_=acc_gate[:], func=ACT.Tanh, bias=bias_gate[:, j : j + 1], scale=0.5
+                    out=gate[:], in_=acc[:], func=ACT.Tanh, bias=bias_gate[:, 2 * a + e : 2 * a + e + 1], scale=0.5
                 )
-
-                nc.vector.tensor_tensor(out=cand[:], in0=cand[:], in1=rec[:], op=ALU.add)
-                nc.vector.tensor_tensor(out=cand[:], in0=cand[:], in1=hx_t[:, :, 2 * u_hx + e], op=ALU.subtract)
                 nc.vector.scalar_tensor_tensor(
-                    out=blend[:, e, :], in0=gate[:], scalar=1.0, in1=cand[:], op0=ALU.add, op1=ALU.mult
+                    out=blend[:, e, :], in0=gate[:], scalar=1.0, in1=cand[:, e, :], op0=ALU.add, op1=ALU.mult
                 )
             return blend
 
         out_dram = out.rearrange("(p n) h -> p n h", n=ROWS)
 
         def finish(c, a, blend, queue):
-            out_rows = work.tile([P, CHUNK_ROWS, 2 * P], F32, name="out_rows")
+            out_rows = work.tile([P, CHUNK_ROWS, 2 * P], F32, name="out_rows", bufs=2)
             features = slice(2 * P * a, 2 * P * (a + 1))
             for half in range(2):
                 bank = psum_t.tile([P, 2, 2, P], F32, name="bank")
@@ -249,7 +262,8 @@ def tile_cfccell_pa_kernel(
                 out=out_dram[:, CHUNK_ROWS * c : CHUNK_ROWS * (c + 1), features], in_=out_rows[:]
             )
 
-        prepare_units(0, HEAD)
+        for i in range(HEAD):
+            quantise(prepare_units(i, 1, False))
 
         bank = psum_t.tile([P, 2, 2, P], F32, name="bank")
         nc.tensor.transpose(bank[:, 0, 0, :], bias_rows[:].bitcast(F32), ident[:])
@@ -266,17 +280,17 @@ def tile_cfccell_pa_kernel(
         step = 0
         for c in range(CHUNKS):
             for a in range(PAIRS):
-                first_layer_pair(c, a)
-                prepare_units(HEAD + PER_STEP * step, PER_STEP)
+                ff2_ready = first_layer_pair(c, a)
+                quantise(prepare_units(HEAD + PER_STEP * step, PER_STEP, True) + ff2_ready)
                 step += 1
         waiting = None
         for a in range(PAIRS):
             for c in range(CHUNKS):
                 blend = blend_pair(c, a)
-                prepare_units(HEAD + PER_STEP * step, PER_STEP)
-                step += 1
                 if waiting is not None:
-                    finish(*waiting)
-                loads_left = HEAD + PER_STEP * (step + 1) < len(units)
-                waiting = (c, a, blend, nc.gpsimd if loads_left else nc.sync)
-        finish(*waiting)
+                    loads_left = HEAD + PER_STEP * step < len(units)
+                    finish(*waiting, nc.gpsimd if loads_left else nc.sync)
+                quantise(prepare_units(HEAD + PER_STEP * step, PER_STEP, False))
+                step += 1
+                waiting = (c, a, blend)
+        finish(*waiting, nc.sync)

@@ -26,7 +26,7 @@ TILES = 2 * PAIRS
 UNIT = 2048
 UNIT_COLS = UNIT // 4
 
-HEAD = 4
+HEAD = 5
 PER_STEP = 2
 
 
@@ -37,10 +37,9 @@ def tile_cfccell_pa_kernel(
     with ExitStack() as ctx:
         keep = ctx.enter_context(tc.tile_pool(name="keep", bufs=1))
         stream = ctx.enter_context(tc.tile_pool(name="stream", bufs=8))
-        stage = ctx.enter_context(tc.tile_pool(name="stage", bufs=5))
+        stage = ctx.enter_context(tc.tile_pool(name="stage", bufs=6))
         work = ctx.enter_context(tc.tile_pool(name="work", bufs=3))
-        psum_t = ctx.enter_context(tc.psum_pool(name="psum_t", bufs=5))
-        psum_z = ctx.enter_context(tc.psum_pool(name="psum_z", bufs=3))
+        psum = ctx.enter_context(tc.psum_pool(name="psum", bufs=8))
         ctx.enter_context(tc.manual_schedule())
 
         ident = keep.tile([P, P], F32, name="ident")
@@ -97,7 +96,7 @@ def tile_cfccell_pa_kernel(
         def transpose_unit(blocks, grouped, vector_helps):
             words = grouped[:].bitcast(F32).rearrange("p (b r u) -> p b r u", b=4, u=2)
             for half in range(2):
-                bank = psum_t.tile([P, 2, 2, P], F32, name="bank")
+                bank = psum.tile([P, 2, 2, P], F32, name="bank", tag="bank")
                 for b in range(2):
                     for u in range(2):
                         nc.tensor.transpose(bank[:, b, u, :], blocks[:, 2 * half + b, u, :], ident[:])
@@ -169,9 +168,9 @@ def tile_cfccell_pa_kernel(
                 units.append(input_weight_unit(a // 2))
             units += [weight_unit(W_r, wr_q, a), weight_unit(W_ta, wta_q, a), weight_unit(W_tb, wtb_q, a)]
 
-        def prepare_units(first, count, vector_helps):
+        def prepare_units(first, count, vector_every):
             return [
-                prepare(*args, vector_helps and i % 2 == 1)
+                prepare(*args, vector_every > 0 and (i + 1) % vector_every == 0)
                 for i, (prepare, args) in enumerate(units[first : first + count])
             ]
 
@@ -182,7 +181,7 @@ def tile_cfccell_pa_kernel(
             if u == 0:
                 ff2_rows[c, g2] = work.tile([P, 4, CHUNK], BF16, name="ff2_rows", bufs=2)
             for e in range(2):
-                acc = psum_z.tile([P, CHUNK], F32, name="acc")
+                acc = psum.tile([P, CHUNK], F32, name="acc", tag="bank")
                 for g in range(2):
                     mx_pass(acc, stationary(wff2_q, a, e, g), moving(ff1_q, c, g), g == 0, g == 1)
                 nc.scalar.activation(
@@ -200,11 +199,11 @@ def tile_cfccell_pa_kernel(
             )
             return [(grouped, moving(ff2_q, c, g2))]
 
-        def blend_pair(c, a):
+        def blend_pair(c, a, ready):
             tiles = range(2)
-            cand = work.tile([P, 2, CHUNK], F32, name="cand")
+            cand = work.tile([P, 2, CHUNK], F32, name="cand", bufs=2)
             for e in tiles:
-                acc = psum_z.tile([P, CHUNK], F32, name="acc")
+                acc = psum.tile([P, CHUNK], F32, name="acc", tag="bank")
                 mx_pass(acc, columns(win_q, P * (2 * a + e), P), moving(x_q, c, 0), True, True)
                 nc.scalar.activation(
                     out=cand[:, e, :], in_=acc[:], func=ACT.Gelu, bias=bias_cand[:, 2 * a + e : 2 * a + e + 1]
@@ -214,8 +213,9 @@ def tile_cfccell_pa_kernel(
             nc.vector.tensor_tensor(
                 out=cand[:], in0=cand[:], in1=hx_t[:, 2 * u_hx : 2 * u_hx + 2, :], op=ALU.subtract
             )
+            quantise(ready[:1])
             for e in tiles:
-                acc = psum_z.tile([P, CHUNK], F32, name="acc")
+                acc = psum.tile([P, CHUNK], F32, name="acc", tag="bank")
                 for g in range(2):
                     mx_pass(acc, stationary(wr_q, a, e, g), moving(hx_q, c, g), g == 0, g == 1)
                 rec = work.tile([P, CHUNK], F32, name="rec")
@@ -223,9 +223,10 @@ def tile_cfccell_pa_kernel(
                     out=rec[:], in_=acc[:], func=ACT.Gelu, bias=bias[:, 5, 2 * a + e : 2 * a + e + 1]
                 )
                 nc.vector.tensor_tensor(out=cand[:, e, :], in0=cand[:, e, :], in1=rec[:], op=ALU.add)
+            quantise(ready[1:])
             blend = work.tile([P, 2, CHUNK], F32, name="blend")
             for e in tiles:
-                acc = psum_z.tile([P, CHUNK], F32, name="acc")
+                acc = psum.tile([P, CHUNK], F32, name="acc", tag="bank")
                 for i, w_q in enumerate((wta_q, wtb_q)):
                     for g in range(2):
                         mx_pass(acc, stationary(w_q, a, e, g), moving(ff2_q, c, g), i + g == 0, i + g == 2)
@@ -240,15 +241,21 @@ def tile_cfccell_pa_kernel(
 
         out_dram = out.rearrange("(p n) h -> p n h", n=ROWS)
 
-        def finish(c, a, blend, queue):
-            out_rows = work.tile([P, CHUNK_ROWS, 2 * P], F32, name="out_rows", bufs=2)
-            features = slice(2 * P * a, 2 * P * (a + 1))
+        def transpose_back(blend):
+            banks = []
             for half in range(2):
-                bank = psum_t.tile([P, 2, 2, P], F32, name="bank")
+                bank = psum.tile([P, 2, 2, P], F32, name="bank", tag="bank")
                 for e in range(2):
                     for n in range(2):
                         r = P * (2 * half + n)
                         nc.tensor.transpose(bank[:, e, n, :], blend[:, e, r : r + P], ident[:])
+                banks.append(bank)
+            return banks
+
+        def add_state_and_store(c, a, banks, queue):
+            out_rows = work.tile([P, CHUNK_ROWS, 2 * P], F32, name="out_rows", bufs=2)
+            features = slice(2 * P * a, 2 * P * (a + 1))
+            for half, bank in enumerate(banks):
                 first = CHUNK_ROWS * c + 2 * half
                 nc.vector.scalar_tensor_tensor(
                     out=out_rows[:, 2 * half : 2 * half + 2, :].rearrange("b n (p e) -> b n p e", e=2),
@@ -263,9 +270,9 @@ def tile_cfccell_pa_kernel(
             )
 
         for i in range(HEAD):
-            quantise(prepare_units(i, 1, False))
+            quantise(prepare_units(i, 1, 1))
 
-        bank = psum_t.tile([P, 2, 2, P], F32, name="bank")
+        bank = psum.tile([P, 2, 2, P], F32, name="bank", tag="bank")
         nc.tensor.transpose(bank[:, 0, 0, :], bias_rows[:].bitcast(F32), ident[:])
         bias_pairs = keep.tile([P, 2 * P], BF16, name="bias_pairs")
         nc.vector.tensor_copy(out=bias_pairs[:].bitcast(F32), in_=bank[:, 0, 0, :])
@@ -277,20 +284,27 @@ def tile_cfccell_pa_kernel(
         bias_cand = keep.tile([P, TILES], F32, name="bias_cand")
         nc.vector.tensor_tensor(out=bias_cand[:], in0=bias[:, 3, :], in1=bias[:, 4, :], op=ALU.add)
 
+        ready = []
         step = 0
         for c in range(CHUNKS):
             for a in range(PAIRS):
+                quantise(ready)
                 ff2_ready = first_layer_pair(c, a)
-                quantise(prepare_units(HEAD + PER_STEP * step, PER_STEP, True) + ff2_ready)
+                ready = prepare_units(HEAD + PER_STEP * step, PER_STEP, 2) + ff2_ready
                 step += 1
-        waiting = None
+        blended = None
+        returned = None
         for a in range(PAIRS):
             for c in range(CHUNKS):
-                blend = blend_pair(c, a)
-                if waiting is not None:
+                if returned is not None:
                     loads_left = HEAD + PER_STEP * step < len(units)
-                    finish(*waiting, nc.gpsimd if loads_left else nc.sync)
-                quantise(prepare_units(HEAD + PER_STEP * step, PER_STEP, False))
+                    add_state_and_store(*returned, nc.gpsimd if loads_left else nc.sync)
+                blend = blend_pair(c, a, ready)
+                ready = prepare_units(HEAD + PER_STEP * step, PER_STEP, 0)
                 step += 1
-                waiting = (c, a, blend)
-        finish(*waiting, nc.sync)
+                if blended is not None:
+                    returned = (blended[0], blended[1], transpose_back(blended[2]))
+                blended = (c, a, blend)
+        last = (blended[0], blended[1], transpose_back(blended[2]))
+        add_state_and_store(*returned, nc.sync)
+        add_state_and_store(*last, nc.sync)

@@ -19,6 +19,7 @@ K_PASS = 512
 WORDS = K_PASS // 2
 CHUNK = 512
 CHUNKS = BATCH // CHUNK
+HALF = CHUNK // 2
 ROWS = BATCH // P
 CHUNK_ROWS = CHUNK // P
 PAIRS = HIDDEN // (2 * P)
@@ -201,41 +202,51 @@ def tile_cfccell_pa_kernel(
 
         def blend_pair(c, a, ready):
             tiles = range(2)
-            cand = work.tile([P, 2, CHUNK], F32, name="cand", bufs=2)
+            halves = range(2)
+
+            def activate(out_tile, e, acc, func, bias_column, scale):
+                nc.scalar.activation(
+                    out=out_tile[:, :, e, :],
+                    in_=acc[:].rearrange("p (h r) -> p h r", h=2),
+                    func=func,
+                    bias=bias_column[:, 2 * a + e : 2 * a + e + 1],
+                    scale=scale,
+                )
+
+            cand = work.tile([P, 2, 2, HALF], F32, name="cand", bufs=2)
             for e in tiles:
                 acc = psum.tile([P, CHUNK], F32, name="acc", tag="bank")
                 mx_pass(acc, columns(win_q, P * (2 * a + e), P), moving(x_q, c, 0), True, True)
-                nc.scalar.activation(
-                    out=cand[:, e, :], in_=acc[:], func=ACT.Gelu, bias=bias_cand[:, 2 * a + e : 2 * a + e + 1]
-                )
+                activate(cand, e, acc, ACT.Gelu, bias_cand, 1.0)
             g_hx, u_hx = divmod(a, 2)
-            hx_t = hx_grouped[c, g_hx][:].rearrange("p (r t) -> p t r", t=4)
-            nc.vector.tensor_tensor(
-                out=cand[:], in0=cand[:], in1=hx_t[:, 2 * u_hx : 2 * u_hx + 2, :], op=ALU.subtract
-            )
+            hx_t = hx_grouped[c, g_hx][:].rearrange("p (h r t) -> p h t r", h=2, t=4)
+            for h in halves:
+                nc.vector.tensor_tensor(
+                    out=cand[:, h], in0=cand[:, h], in1=hx_t[:, h, 2 * u_hx : 2 * u_hx + 2, :], op=ALU.subtract
+                )
             quantise(ready[:1])
+
+            rec = work.tile([P, 2, 2, HALF], F32, name="rec", bufs=2)
             for e in tiles:
                 acc = psum.tile([P, CHUNK], F32, name="acc", tag="bank")
                 for g in range(2):
                     mx_pass(acc, stationary(wr_q, a, e, g), moving(hx_q, c, g), g == 0, g == 1)
-                rec = work.tile([P, CHUNK], F32, name="rec")
-                nc.scalar.activation(
-                    out=rec[:], in_=acc[:], func=ACT.Gelu, bias=bias[:, 5, 2 * a + e : 2 * a + e + 1]
-                )
-                nc.vector.tensor_tensor(out=cand[:, e, :], in0=cand[:, e, :], in1=rec[:], op=ALU.add)
+                activate(rec, e, acc, ACT.Gelu, bias[:, 5, :], 1.0)
+            for h in halves:
+                nc.vector.tensor_tensor(out=cand[:, h], in0=cand[:, h], in1=rec[:, h], op=ALU.add)
             quantise(ready[1:])
-            blend = work.tile([P, 2, CHUNK], F32, name="blend")
+
+            gate = work.tile([P, 2, 2, HALF], F32, name="gate", bufs=2)
             for e in tiles:
                 acc = psum.tile([P, CHUNK], F32, name="acc", tag="bank")
                 for i, w_q in enumerate((wta_q, wtb_q)):
                     for g in range(2):
                         mx_pass(acc, stationary(w_q, a, e, g), moving(ff2_q, c, g), i + g == 0, i + g == 2)
-                gate = work.tile([P, CHUNK], F32, name="gate")
-                nc.scalar.activation(
-                    out=gate[:], in_=acc[:], func=ACT.Tanh, bias=bias_gate[:, 2 * a + e : 2 * a + e + 1], scale=0.5
-                )
+                activate(gate, e, acc, ACT.Tanh, bias_gate, 0.5)
+            blend = work.tile([P, 2, 2, HALF], F32, name="blend")
+            for h in halves:
                 nc.vector.scalar_tensor_tensor(
-                    out=blend[:, e, :], in0=gate[:], scalar=1.0, in1=cand[:, e, :], op0=ALU.add, op1=ALU.mult
+                    out=blend[:, h], in0=gate[:, h], scalar=1.0, in1=cand[:, h], op0=ALU.add, op1=ALU.mult
                 )
             return blend
 
@@ -247,27 +258,24 @@ def tile_cfccell_pa_kernel(
                 bank = psum.tile([P, 2, 2, P], F32, name="bank", tag="bank")
                 for e in range(2):
                     for n in range(2):
-                        r = P * (2 * half + n)
-                        nc.tensor.transpose(bank[:, e, n, :], blend[:, e, r : r + P], ident[:])
+                        nc.tensor.transpose(bank[:, e, n, :], blend[:, half, e, P * n : P * (n + 1)], ident[:])
                 banks.append(bank)
             return banks
 
         def add_state_and_store(c, a, banks, queue):
-            out_rows = work.tile([P, CHUNK_ROWS, 2 * P], F32, name="out_rows", bufs=2)
             features = slice(2 * P * a, 2 * P * (a + 1))
             for half, bank in enumerate(banks):
                 first = CHUNK_ROWS * c + 2 * half
+                out_rows = work.tile([P, 2, 2 * P], F32, name="out_rows", bufs=4)
                 nc.vector.scalar_tensor_tensor(
-                    out=out_rows[:, 2 * half : 2 * half + 2, :].rearrange("b n (p e) -> b n p e", e=2),
+                    out=out_rows[:].rearrange("b n (p e) -> b n p e", e=2),
                     in0=bank[:].rearrange("b e n p -> b n p e"),
                     scalar=0.5,
                     in1=hx_rows[:, first : first + 2, features].rearrange("b n (p e) -> b n p e", e=2),
                     op0=ALU.mult,
                     op1=ALU.add,
                 )
-            queue.dma_start(
-                out=out_dram[:, CHUNK_ROWS * c : CHUNK_ROWS * (c + 1), features], in_=out_rows[:]
-            )
+                queue.dma_start(out=out_dram[:, first : first + 2, features], in_=out_rows[:])
 
         for i in range(HEAD):
             quantise(prepare_units(i, 1, 1))
@@ -290,7 +298,7 @@ def tile_cfccell_pa_kernel(
             for a in range(PAIRS):
                 quantise(ready)
                 ff2_ready = first_layer_pair(c, a)
-                ready = prepare_units(HEAD + PER_STEP * step, PER_STEP, 2) + ff2_ready
+                ready = ff2_ready + prepare_units(HEAD + PER_STEP * step, PER_STEP, 2)
                 step += 1
         blended = None
         returned = None

@@ -123,24 +123,23 @@ def tile_cfccell_pa_kernel(
             transpose_unit(blocks, grouped, vector_helps)
             return grouped, dest
 
-        hx_nat = keep.tile([P, ROWS * HIDDEN], BF16, name="hx_nat")
-        hx_rows = hx_nat[:].rearrange("p (n k) -> p n k", n=ROWS)
-        hx_words = hx_nat[:].bitcast(F32).rearrange("p (n w) -> p n w", n=ROWS)
         hx_dram = hx.rearrange("(p n) k -> p n k", n=ROWS)
+        hx_nat = []
         hx_grouped = {}
         for c in range(CHUNKS):
+            hx_nat.append(keep.tile([P, CHUNK_ROWS, HIDDEN], BF16, name="hx_nat_%d" % c))
             for g in range(2):
                 hx_grouped[c, g] = keep.tile(
                     [P, UNIT], BF16, name="hx_grouped_%d_%d" % (c, g), align_bytes=64
                 )
 
         def prepare_state(c, g, vector_helps):
-            rows = slice(CHUNK_ROWS * c, CHUNK_ROWS * (c + 1))
-            ks = slice(K_PASS * g, K_PASS * (g + 1))
-            nc.sync.dma_start(out=hx_rows[:, rows, ks], in_=hx_dram[:, rows, ks])
-            blocks = hx_words[:, rows, WORDS * g : WORDS * (g + 1)].rearrange(
-                "p n (u w) -> p n u w", u=2
-            )
+            if g == 0:
+                rows = slice(CHUNK_ROWS * c, CHUNK_ROWS * (c + 1))
+                nc.sync.dma_start(out=hx_nat[c][:], in_=hx_dram[:, rows, :])
+            blocks = hx_nat[c][:].rearrange("p n k -> p (n k)").bitcast(F32).rearrange(
+                "p (n g u w) -> p g n u w", n=CHUNK_ROWS, g=2, u=2
+            )[:, g]
             transpose_unit(blocks, hx_grouped[c, g], vector_helps)
             return hx_grouped[c, g], moving(hx_q, c, g)
 
@@ -271,7 +270,7 @@ def tile_cfccell_pa_kernel(
                     out=out_rows[:].rearrange("b n (p e) -> b n p e", e=2),
                     in0=bank[:].rearrange("b e n p -> b n p e"),
                     scalar=0.5,
-                    in1=hx_rows[:, first : first + 2, features].rearrange("b n (p e) -> b n p e", e=2),
+                    in1=hx_nat[c][:, 2 * half : 2 * half + 2, features].rearrange("b n (p e) -> b n p e", e=2),
                     op0=ALU.mult,
                     op1=ALU.add,
                 )

@@ -16,19 +16,22 @@ BATCH, IN_FEATURES, HIDDEN = 1024, 512, 1024
 FLOPS = 2 * BATCH * HIDDEN * (4 * HIDDEN + IN_FEATURES)
 
 K_PASS = 512
-WORDS = K_PASS // 2
 CHUNK = 512
 CHUNKS = BATCH // CHUNK
 HALF = CHUNK // 2
 ROWS = BATCH // P
 CHUNK_ROWS = CHUNK // P
+HALF_ROWS = HALF // P
 PAIRS = HIDDEN // (2 * P)
 TILES = 2 * PAIRS
 UNIT = 2048
 UNIT_COLS = UNIT // 4
 
-HEAD = 5
-PER_STEP = 2
+PROGRAM = "UqUqUqUqUqBqFuUqFiuUqFuUqFiuUqFuUqFiuUqFuUqFiuUCsqRaGmuuCsqRaGmuboCsqRaGmuuboCsqRaGmuboCsqRaGmuboCsqRaGmboCsqRaGmboCsqRaGmbobo"
+SPLIT = True
+GPI = 0
+WARM0 = 0
+WN = [512]
 
 
 def tile_cfccell_pa_kernel(
@@ -39,23 +42,31 @@ def tile_cfccell_pa_kernel(
         keep = ctx.enter_context(tc.tile_pool(name="keep", bufs=1))
         stream = ctx.enter_context(tc.tile_pool(name="stream", bufs=8))
         stage = ctx.enter_context(tc.tile_pool(name="stage", bufs=6))
-        work = ctx.enter_context(tc.tile_pool(name="work", bufs=3))
+        work = ctx.enter_context(tc.tile_pool(name="work", bufs=2))
         psum = ctx.enter_context(tc.psum_pool(name="psum", bufs=8))
         ctx.enter_context(tc.manual_schedule())
 
+        warm_in = keep.tile([P, CHUNK], BF16, name="warm_in")
+        nc.vector.memset(warm_in[:], 0.0)
         ident = keep.tile([P, P], F32, name="ident")
         make_identity(nc, ident[:])
+        table = keep.tile([P, 1], F32, name="table")
+        nc.vector.memset(table[:], 0.0)
+        nc.scalar.activation(out=table[:], in_=table[:], func=ACT.Gelu)
 
-        warm = keep.tile([P, 1], F32, name="warm")
-        nc.vector.memset(warm[:], 0.0)
-        nc.scalar.activation(out=warm[:], in_=warm[:], func=ACT.Gelu)
+        def warm(sizes):
+            for n in sizes:
+                bank = psum.tile([P, CHUNK], F32, name="idle", tag="bank")
+                nc.tensor.matmul(bank[:, 0:n], lhsT=warm_in[:, 0:P], rhs=warm_in[:, 0:n], start=True, stop=True)
 
         bias_rows = keep.tile([P, 2 * P], BF16, name="bias_rows")
         nc.vector.memset(bias_rows[:], 0.0)
-        for v, vector in enumerate((b_ff2, b_ta, b_tb, b_in, input_b, r_b)):
-            nc.scalar.dma_start(
+        vectors = [b_ff2, b_ta, b_tb, b_in, input_b, r_b]
+
+        def load_bias(v):
+            nc.sync.dma_start(
                 out=bias_rows[PAIRS * v : PAIRS * (v + 1), :],
-                in_=vector.rearrange("(a w) -> a w", a=PAIRS),
+                in_=vectors[v].rearrange("(a w) -> a w", a=PAIRS),
             )
 
         def mx_operand(name, width):
@@ -77,15 +88,15 @@ def tile_cfccell_pa_kernel(
         wr_q = mx_operand("wr", 2 * HIDDEN)
         win_q = mx_operand("win", HIDDEN)
 
-        def moving(operand, c, g):
-            return columns(operand, BATCH * g + CHUNK * c, CHUNK)
+        def moving(operand, c, g, first=0, count=CHUNK):
+            return columns(operand, BATCH * g + CHUNK * c + first, count)
 
         def stationary(operand, a, e, g):
             return columns(operand, UNIT_COLS * a + P * (2 * e + g), P)
 
         def mx_pass(acc, weights, acts, start, stop):
             nc.tensor.matmul_mx(
-                out=acc[:],
+                out=acc,
                 lhsT=weights[0].bitcast(FP8X4),
                 lhsT_scale=weights[1],
                 rhs=acts[0].bitcast(FP8X4),
@@ -100,7 +111,7 @@ def tile_cfccell_pa_kernel(
                 bank = psum.tile([P, 2, 2, P], F32, name="bank", tag="bank")
                 for b in range(2):
                     for u in range(2):
-                        nc.tensor.transpose(bank[:, b, u, :], blocks[:, 2 * half + b, u, :], ident[:])
+                        nc.tensor.transpose(bank[:, b, u, :], blocks[2 * half + b][:, u, :], ident[:])
                 copy_out = nc.vector.tensor_copy if vector_helps and half == 1 else nc.scalar.copy
                 copy_out(
                     out=words[:, 2 * half : 2 * half + 2, :, :],
@@ -108,210 +119,281 @@ def tile_cfccell_pa_kernel(
                 )
 
         def quantise(ready):
-            for grouped, (codes, scales) in ready:
-                nc.vector.quantize_mx(out=codes.bitcast(FP8X4), scales=scales, in_=grouped[:])
+            for source, (codes, scales) in ready:
+                nc.vector.quantize_mx(out=codes.bitcast(FP8X4), scales=scales, in_=source)
 
-        def prepare_streamed(pieces, dest, vector_helps):
-            raw = stream.tile([P, UNIT], BF16, name="raw")
-            landing = raw[:].rearrange("p (b k) -> p b k", b=4)
-            first = 0
-            for piece in pieces:
-                nc.sync.dma_start(out=landing[:, first : first + piece.shape[1], :], in_=piece)
-                first += piece.shape[1]
-            grouped = stage.tile([P, UNIT], BF16, name="grouped", align_bytes=64)
-            blocks = raw[:].bitcast(F32).rearrange("p (b u w) -> p b u w", b=4, u=2)
-            transpose_unit(blocks, grouped, vector_helps)
-            return grouped, dest
+        def new_grouped():
+            return stage.tile([P, UNIT], BF16, name="grouped", align_bytes=64)
 
-        hx_dram = hx.rearrange("(p n) k -> p n k", n=ROWS)
-        hx_nat = []
-        hx_grouped = {}
-        for c in range(CHUNKS):
-            hx_nat.append(keep.tile([P, CHUNK_ROWS, HIDDEN], BF16, name="hx_nat_%d" % c))
-            for g in range(2):
-                hx_grouped[c, g] = keep.tile(
-                    [P, UNIT], BF16, name="hx_grouped_%d_%d" % (c, g), align_bytes=64
-                )
+        def weight_unit(pieces, dest):
+            def load():
+                raw = stream.tile([P, 4, K_PASS], BF16, name="raw")
+                first = 0
+                for piece in pieces:
+                    nc.sync.dma_start(out=raw[:, first : first + piece.shape[1], :], in_=piece)
+                    first += piece.shape[1]
+                return raw
 
-        def prepare_state(c, g, vector_helps):
-            if g == 0:
-                rows = slice(CHUNK_ROWS * c, CHUNK_ROWS * (c + 1))
-                nc.sync.dma_start(out=hx_nat[c][:], in_=hx_dram[:, rows, :])
-            blocks = hx_nat[c][:].rearrange("p n k -> p (n k)").bitcast(F32).rearrange(
-                "p (n g u w) -> p g n u w", n=CHUNK_ROWS, g=2, u=2
-            )[:, g]
-            transpose_unit(blocks, hx_grouped[c, g], vector_helps)
-            return hx_grouped[c, g], moving(hx_q, c, g)
+            def prepare(raw, vector_helps):
+                grouped = new_grouped()
+                words = raw[:].rearrange("p b k -> p (b k)").bitcast(F32).rearrange("p (b u w) -> p b u w", b=4, u=2)
+                transpose_unit([words[:, b] for b in range(4)], grouped, vector_helps)
+                return [(grouped[:], dest)]
 
-        def activation_unit(source, operand, c, g):
-            rows = source.rearrange("(p n) k -> p n k", n=ROWS)[
-                :, CHUNK_ROWS * c : CHUNK_ROWS * (c + 1), K_PASS * g : K_PASS * (g + 1)
-            ]
-            return prepare_streamed, ([rows], moving(operand, c, g))
+            return load, prepare
 
-        def weight_unit(source, operand, a):
-            rows = source.rearrange("(a p e) k -> a p (e k)", p=P, e=2)[a]
-            blocks = rows.rearrange("p (b k) -> p b k", b=4)
-            return prepare_streamed, ([blocks], columns(operand, UNIT_COLS * a, UNIT_COLS))
+        def pair_weights(source, operand, a, cut=1):
+            rows = source.rearrange("(a p e) k -> a p (e k)", p=P, e=2)[a].rearrange("p (b k) -> p b k", b=4)
+            n = 4 // cut
+            return weight_unit([rows[:, n * i : n * (i + 1)] for i in range(cut)], columns(operand, UNIT_COLS * a, UNIT_COLS))
 
-        def input_weight_unit(h):
+        def input_weights(h):
             rows = W_in.rearrange("(a p e) k -> a p e k", p=P, e=2)
-            return prepare_streamed, ([rows[2 * h], rows[2 * h + 1]], columns(win_q, UNIT_COLS * h, UNIT_COLS))
+            return weight_unit([rows[2 * h], rows[2 * h + 1]], columns(win_q, UNIT_COLS * h, UNIT_COLS))
 
-        units = [activation_unit(ff1, ff1_q, 0, g) for g in range(2)]
-        units += [weight_unit(W_ff2, wff2_q, a) for a in range(PAIRS)]
-        units += [activation_unit(ff1, ff1_q, 1, g) for g in range(2)]
-        units += [activation_unit(x, x_q, c, 0) for c in range(CHUNKS)]
-        units += [(prepare_state, (c, g)) for c in range(CHUNKS) for g in range(2)]
+        def input_rows(c):
+            rows = x.rearrange("(p n) k -> p n k", n=ROWS)[:, CHUNK_ROWS * c : CHUNK_ROWS * (c + 1), :]
+            return weight_unit([rows], moving(x_q, c, 0))
+
+        def half_chunk(source, operand, c, h, tiles, kept):
+            first = CHUNK_ROWS * c + HALF_ROWS * h
+
+            def load():
+                raw = tiles()
+                nc.sync.dma_start(out=raw[:], in_=source.rearrange("(p n) k -> p n k", n=ROWS)[:, first : first + HALF_ROWS, :])
+                return raw
+
+            def prepare(raw, vector_helps):
+                grouped = kept if kept is not None else new_grouped()
+                words = raw[:].rearrange("p n k -> p (n k)").bitcast(F32).rearrange("p (n g u w) -> p g n u w", n=HALF_ROWS, g=2, u=2)
+                transpose_unit([words[:, g, n] for g in range(2) for n in range(HALF_ROWS)], grouped, vector_helps)
+                return [
+                    (grouped[:, 4 * HALF * g : 4 * HALF * (g + 1)], moving(operand, c, g, HALF * h, HALF))
+                    for g in range(2)
+                ]
+
+            return load, prepare
+
+        hx_nat = {}
+        hx_grouped = {}
+
+        def backbone_half(c, h):
+            return half_chunk(ff1, ff1_q, c, h, lambda: stream.tile([P, HALF_ROWS, HIDDEN], BF16, name="raw"), None)
+
+        def state_half(c, h):
+            hx_nat[c, h] = keep.tile([P, HALF_ROWS, HIDDEN], BF16, name="hx_nat_%d_%d" % (c, h))
+            hx_grouped[c, h] = keep.tile([P, UNIT], BF16, name="hx_grouped_%d_%d" % (c, h), align_bytes=64)
+            return half_chunk(hx, hx_q, c, h, lambda: hx_nat[c, h], hx_grouped[c, h])
+
+        units = [pair_weights(W_ff2, wff2_q, 0, 2)]
+        units += [backbone_half(0, h) for h in range(2)]
+        units += [pair_weights(W_ff2, wff2_q, a) for a in range(1, PAIRS)]
+        units += [backbone_half(1, h) for h in range(2)]
+        units += [input_rows(c) for c in range(CHUNKS)]
+        units += [state_half(c, h) for c in range(CHUNKS) for h in range(2)]
         for a in range(PAIRS):
             if a % 2 == 0:
-                units.append(input_weight_unit(a // 2))
-            units += [weight_unit(W_r, wr_q, a), weight_unit(W_ta, wta_q, a), weight_unit(W_tb, wtb_q, a)]
-
-        def prepare_units(first, count, vector_every):
-            return [
-                prepare(*args, vector_every > 0 and (i + 1) % vector_every == 0)
-                for i, (prepare, args) in enumerate(units[first : first + count])
-            ]
+                units.append(input_weights(a // 2))
+            units += [pair_weights(W_r, wr_q, a), pair_weights(W_ta, wta_q, a), pair_weights(W_tb, wtb_q, a)]
 
         ff2_rows = {}
 
         def first_layer_pair(c, a):
             g2, u = divmod(a, 2)
             if u == 0:
-                ff2_rows[c, g2] = work.tile([P, 4, CHUNK], BF16, name="ff2_rows", bufs=2)
+                ff2_rows[c, g2] = work.tile([P, 4, CHUNK], BF16, name="ff2_rows")
             for e in range(2):
                 acc = psum.tile([P, CHUNK], F32, name="acc", tag="bank")
                 for g in range(2):
-                    mx_pass(acc, stationary(wff2_q, a, e, g), moving(ff1_q, c, g), g == 0, g == 1)
+                    mx_pass(acc[:], stationary(wff2_q, a, e, g), moving(ff1_q, c, g), g == 0, g == 1)
                 nc.scalar.activation(
                     out=ff2_rows[c, g2][:, 2 * u + e, :],
                     in_=acc[:],
                     func=ACT.Gelu,
                     bias=bias[:, 0, 2 * a + e : 2 * a + e + 1],
                 )
-            if u == 0:
-                return []
-            grouped = stage.tile([P, UNIT], BF16, name="grouped", align_bytes=64)
-            nc.vector.tensor_copy(
-                out=grouped[:].rearrange("p (r t) -> p r t", t=4),
-                in_=ff2_rows[c, g2][:].rearrange("p t r -> p r t"),
+            return [(c, g2)] if u == 1 else []
+
+        def interleave(c, g2):
+            grouped = new_grouped()
+            if GPI:
+                n = CHUNK // GPI
+                for q in range(GPI):
+                    nc.gpsimd.tensor_scalar(
+                        out=grouped[:, 4 * n * q : 4 * n * (q + 1)].rearrange("p (r t) -> p r t", t=4),
+                        in0=ff2_rows[c, g2][:, :, n * q : n * (q + 1)].rearrange("p t r -> p r t"),
+                        scalar1=1.0,
+                        scalar2=0.0,
+                        op0=ALU.mult,
+                        op1=ALU.add,
+                    )
+            else:
+                nc.vector.tensor_copy(
+                    out=grouped[:].rearrange("p (r t) -> p r t", t=4),
+                    in_=ff2_rows[c, g2][:].rearrange("p t r -> p r t"),
+                )
+            return [(grouped[:], moving(ff2_q, c, g2))]
+
+        def activate(out_tile, a, e, acc, func, bias_column, scale):
+            nc.scalar.activation(
+                out=out_tile[:, :, e, :],
+                in_=acc[:].rearrange("p (h r) -> p h r", h=2),
+                func=func,
+                bias=bias_column[:, 2 * a + e : 2 * a + e + 1],
+                scale=scale,
             )
-            return [(grouped, moving(ff2_q, c, g2))]
 
-        def blend_pair(c, a, ready):
-            tiles = range(2)
-            halves = range(2)
-
-            def activate(out_tile, e, acc, func, bias_column, scale):
-                nc.scalar.activation(
-                    out=out_tile[:, :, e, :],
-                    in_=acc[:].rearrange("p (h r) -> p h r", h=2),
-                    func=func,
-                    bias=bias_column[:, 2 * a + e : 2 * a + e + 1],
-                    scale=scale,
-                )
-
-            cand = work.tile([P, 2, 2, HALF], F32, name="cand", bufs=2)
-            for e in tiles:
+        def input_product(c, a):
+            cand = work.tile([P, 2, 2, HALF], F32, name="cand", bufs=3)
+            for e in range(2):
                 acc = psum.tile([P, CHUNK], F32, name="acc", tag="bank")
-                mx_pass(acc, columns(win_q, P * (2 * a + e), P), moving(x_q, c, 0), True, True)
-                activate(cand, e, acc, ACT.Gelu, bias_cand, 1.0)
-            g_hx, u_hx = divmod(a, 2)
-            hx_t = hx_grouped[c, g_hx][:].rearrange("p (h r t) -> p h t r", h=2, t=4)
-            for h in halves:
-                nc.vector.tensor_tensor(
-                    out=cand[:, h], in0=cand[:, h], in1=hx_t[:, h, 2 * u_hx : 2 * u_hx + 2, :], op=ALU.subtract
-                )
-            quantise(ready[:1])
+                mx_pass(acc[:], columns(win_q, P * (2 * a + e), P), moving(x_q, c, 0), True, True)
+                activate(cand, a, e, acc, ACT.Gelu, bias_cand, 1.0)
+            return cand
 
-            rec = work.tile([P, 2, 2, HALF], F32, name="rec", bufs=2)
-            for e in tiles:
+        def state_product(c, a):
+            rec = work.tile([P, 2, 2, HALF], F32, name="rec")
+            for e in range(2):
                 acc = psum.tile([P, CHUNK], F32, name="acc", tag="bank")
                 for g in range(2):
-                    mx_pass(acc, stationary(wr_q, a, e, g), moving(hx_q, c, g), g == 0, g == 1)
-                activate(rec, e, acc, ACT.Gelu, bias[:, 5, :], 1.0)
-            for h in halves:
-                nc.vector.tensor_tensor(out=cand[:, h], in0=cand[:, h], in1=rec[:, h], op=ALU.add)
-            quantise(ready[1:])
+                    mx_pass(acc[:], stationary(wr_q, a, e, g), moving(hx_q, c, g), g == 0, g == 1)
+                activate(rec, a, e, acc, ACT.Gelu, bias[:, 5, :], 1.0)
+            return rec
 
-            gate = work.tile([P, 2, 2, HALF], F32, name="gate", bufs=2)
-            for e in tiles:
+        gate_terms = [(wta_q, 0), (wta_q, 1), (wtb_q, 0), (wtb_q, 1)]
+
+        def gate_product(c, a):
+            gate = work.tile([P, 2, 2, HALF], F32, name="gate")
+            for e in range(2):
                 acc = psum.tile([P, CHUNK], F32, name="acc", tag="bank")
-                for i, w_q in enumerate((wta_q, wtb_q)):
-                    for g in range(2):
-                        mx_pass(acc, stationary(w_q, a, e, g), moving(ff2_q, c, g), i + g == 0, i + g == 2)
-                activate(gate, e, acc, ACT.Tanh, bias_gate, 0.5)
-            blend = work.tile([P, 2, 2, HALF], F32, name="blend")
-            for h in halves:
-                nc.vector.scalar_tensor_tensor(
-                    out=blend[:, h], in0=gate[:, h], scalar=1.0, in1=cand[:, h], op0=ALU.add, op1=ALU.mult
+                for i, (w_q, g) in enumerate(gate_terms):
+                    mx_pass(acc[:], stationary(w_q, a, e, g), moving(ff2_q, c, g), i == 0, i == 3)
+                activate(gate, a, e, acc, ACT.Tanh, bias_gate, 0.5)
+            return gate
+
+        def gate_product_by_halves(c, a):
+            gate = work.tile([P, 2, 2, HALF], F32, name="gate")
+            for h in range(2):
+                acc = psum.tile([P, 2, HALF], F32, name="acc", tag="bank")
+                for e in range(2):
+                    for i, (w_q, g) in enumerate(gate_terms):
+                        mx_pass(acc[:, e, :], stationary(w_q, a, e, g), moving(ff2_q, c, g, HALF * h, HALF), i == 0, i == 3)
+                for e in range(2):
+                    nc.scalar.activation(
+                        out=gate[:, h, e, :],
+                        in_=acc[:, e, :],
+                        func=ACT.Tanh,
+                        bias=bias_gate[:, 2 * a + e : 2 * a + e + 1],
+                        scale=0.5,
+                    )
+            return gate
+
+        def subtract_state(c, a, cand):
+            g_hx, u_hx = divmod(a, 2)
+            for h in range(2):
+                hx_t = hx_grouped[c, h][:].rearrange("p (g r t) -> p g t r", g=2, t=4)
+                nc.vector.tensor_tensor(
+                    out=cand[:, h], in0=cand[:, h], in1=hx_t[:, g_hx, 2 * u_hx : 2 * u_hx + 2, :], op=ALU.subtract
                 )
-            return blend
+
+        def add_rec(cand, rec):
+            for h in range(2):
+                nc.vector.tensor_tensor(out=cand[:, h], in0=cand[:, h], in1=rec[:, h], op=ALU.add)
+
+        def multiply(cand, gate, blend, h):
+            nc.vector.scalar_tensor_tensor(
+                out=blend[:, h], in0=gate[:, h], scalar=1.0, in1=cand[:, h], op0=ALU.add, op1=ALU.mult
+            )
 
         out_dram = out.rearrange("(p n) h -> p n h", n=ROWS)
 
-        def transpose_back(blend):
-            banks = []
-            for half in range(2):
-                bank = psum.tile([P, 2, 2, P], F32, name="bank", tag="bank")
-                for e in range(2):
-                    for n in range(2):
-                        nc.tensor.transpose(bank[:, e, n, :], blend[:, half, e, P * n : P * (n + 1)], ident[:])
-                banks.append(bank)
-            return banks
+        def transpose_back(blend, half):
+            bank = psum.tile([P, 2, 2, P], F32, name="bank", tag="bank")
+            for e in range(2):
+                for n in range(2):
+                    nc.tensor.transpose(bank[:, e, n, :], blend[:, half, e, P * n : P * (n + 1)], ident[:])
+            return bank
 
-        def add_state_and_store(c, a, banks, queue):
+        def add_state_and_store(c, a, half, bank, queue):
             features = slice(2 * P * a, 2 * P * (a + 1))
-            for half, bank in enumerate(banks):
-                first = CHUNK_ROWS * c + 2 * half
-                out_rows = work.tile([P, 2, 2 * P], F32, name="out_rows", bufs=4)
-                nc.vector.scalar_tensor_tensor(
-                    out=out_rows[:].rearrange("b n (p e) -> b n p e", e=2),
-                    in0=bank[:].rearrange("b e n p -> b n p e"),
-                    scalar=0.5,
-                    in1=hx_nat[c][:, 2 * half : 2 * half + 2, features].rearrange("b n (p e) -> b n p e", e=2),
-                    op0=ALU.mult,
-                    op1=ALU.add,
-                )
-                queue.dma_start(out=out_dram[:, first : first + 2, features], in_=out_rows[:])
+            first = CHUNK_ROWS * c + 2 * half
+            out_rows = work.tile([P, 2, 2 * P], F32, name="out_rows", bufs=4)
+            nc.vector.scalar_tensor_tensor(
+                out=out_rows[:].rearrange("b n (p e) -> b n p e", e=2),
+                in0=bank[:].rearrange("b e n p -> b n p e"),
+                scalar=0.5,
+                in1=hx_nat[c, half][:, :, features].rearrange("b n (p e) -> b n p e", e=2),
+                op0=ALU.mult,
+                op1=ALU.add,
+            )
+            queue.dma_start(out=out_dram[:, first : first + 2, features], in_=out_rows[:])
 
-        for i in range(HEAD):
-            quantise(prepare_units(i, 1, 1))
-
-        bank = psum.tile([P, 2, 2, P], F32, name="bank", tag="bank")
-        nc.tensor.transpose(bank[:, 0, 0, :], bias_rows[:].bitcast(F32), ident[:])
-        bias_pairs = keep.tile([P, 2 * P], BF16, name="bias_pairs")
-        nc.vector.tensor_copy(out=bias_pairs[:].bitcast(F32), in_=bank[:, 0, 0, :])
-        bias = keep.tile([P, 6, TILES], F32, name="bias")
-        nc.vector.tensor_copy(out=bias[:].rearrange("p v j -> p (v j)"), in_=bias_pairs[:, 0 : 6 * TILES])
-        bias_gate = keep.tile([P, TILES], F32, name="bias_gate")
-        nc.vector.tensor_tensor(out=bias_gate[:], in0=bias[:, 1, :], in1=bias[:, 2, :], op=ALU.add)
-        nc.vector.tensor_scalar_mul(out=bias_gate[:], in0=bias_gate[:], scalar1=0.5)
-        bias_cand = keep.tile([P, TILES], F32, name="bias_cand")
-        nc.vector.tensor_tensor(out=bias_cand[:], in0=bias[:, 3, :], in1=bias[:, 4, :], op=ALU.add)
-
-        ready = []
-        step = 0
-        for c in range(CHUNKS):
-            for a in range(PAIRS):
-                quantise(ready)
-                ff2_ready = first_layer_pair(c, a)
-                ready = ff2_ready + prepare_units(HEAD + PER_STEP * step, PER_STEP, 2)
-                step += 1
-        blended = None
-        returned = None
-        for a in range(PAIRS):
-            for c in range(CHUNKS):
-                if returned is not None:
-                    loads_left = HEAD + PER_STEP * step < len(units)
-                    add_state_and_store(*returned, nc.gpsimd if loads_left else nc.sync)
-                blend = blend_pair(c, a, ready)
-                ready = prepare_units(HEAD + PER_STEP * step, PER_STEP, 0)
-                step += 1
-                if blended is not None:
-                    returned = (blended[0], blended[1], transpose_back(blended[2]))
-                blended = (c, a, blend)
-        last = (blended[0], blended[1], transpose_back(blended[2]))
-        add_state_and_store(*returned, nc.sync)
-        add_state_and_store(*last, nc.sync)
+        st = {"pos": 0, "bl": list(range(6))}
+        fresh = []
+        rows_done = []
+        F_list = [(c, a) for c in range(CHUNKS) for a in range(PAIRS)]
+        pair_list = [(c, a) for a in range(PAIRS) for c in range(CHUNKS)]
+        lists = {k: list(pair_list) for k in "CRG"}
+        cands, recs, gates, blends = {}, {}, {}, {}
+        sub_l, add_l, mul_l, back_l, out_l = list(pair_list), list(pair_list), list(pair_list), list(pair_list), []
+        warm([CHUNK] * WARM0)
+        for token in PROGRAM:
+            if token in "uUv":
+                load, prepare = units[st["pos"]]
+                raw = load()
+                for v in st["bl"][:2]:
+                    load_bias(v)
+                st["bl"] = st["bl"][2:]
+                fresh += prepare(raw, token == "U")
+                st["pos"] += 1
+            elif token == "q":
+                quantise(fresh)
+                fresh = []
+            elif token == "i":
+                for args in rows_done:
+                    fresh += interleave(*args)
+                rows_done = []
+            elif token == "F":
+                rows_done += first_layer_pair(*F_list.pop(0))
+            elif token == "C":
+                k = lists["C"].pop(0)
+                cands[k] = input_product(*k)
+            elif token == "R":
+                k = lists["R"].pop(0)
+                recs[k] = state_product(*k)
+            elif token == "G":
+                k = lists["G"].pop(0)
+                gates[k] = gate_product_by_halves(*k) if (SPLIT and not lists["G"]) else gate_product(*k)
+            elif token == "s":
+                k = sub_l.pop(0)
+                subtract_state(k[0], k[1], cands[k])
+            elif token == "a":
+                k = add_l.pop(0)
+                add_rec(cands[k], recs[k])
+            elif token == "m":
+                k = mul_l.pop(0)
+                blends[k] = work.tile([P, 2, 2, HALF], F32, name="blend", bufs=3)
+                for h in range(2):
+                    multiply(cands[k], gates[k], blends[k], h)
+            elif token == "b":
+                k = back_l.pop(0)
+                for h in range(2):
+                    out_l.append((k[0], k[1], h, transpose_back(blends[k], h)))
+            elif token == "o":
+                for i in range(2):
+                    add_state_and_store(*out_l.pop(0), nc.gpsimd if st["pos"] < len(units) else nc.sync)
+            elif token == "w":
+                warm([CHUNK])
+            elif token == "B":
+                bank = psum.tile([P, 2, 2, P], F32, name="bank", tag="bank")
+                nc.tensor.transpose(bank[:, 0, 0, :], bias_rows[:].bitcast(F32), ident[:])
+                bias_pairs = keep.tile([P, 2 * P], BF16, name="bias_pairs")
+                nc.vector.tensor_copy(out=bias_pairs[:].bitcast(F32), in_=bank[:, 0, 0, :])
+                bias = keep.tile([P, 6, TILES], F32, name="bias")
+                nc.vector.tensor_copy(out=bias[:].rearrange("p v j -> p (v j)"), in_=bias_pairs[:, 0 : 6 * TILES])
+                bias_gate = keep.tile([P, TILES], F32, name="bias_gate")
+                nc.vector.tensor_tensor(out=bias_gate[:], in0=bias[:, 1, :], in1=bias[:, 2, :], op=ALU.add)
+                nc.vector.tensor_scalar_mul(out=bias_gate[:], in0=bias_gate[:], scalar1=0.5)
+                bias_cand = keep.tile([P, TILES], F32, name="bias_cand")
+                nc.vector.tensor_tensor(out=bias_cand[:], in0=bias[:, 3, :], in1=bias[:, 4, :], op=ALU.add)
+        assert not (fresh or rows_done or out_l or back_l or mul_l or lists["G"] or F_list) and st["pos"] == 28

@@ -27,11 +27,10 @@ TILES = 2 * PAIRS
 UNIT = 2048
 UNIT_COLS = UNIT // 4
 
-PROGRAM = "UqUqUqUqUqBqFuUqFiuUqFuUqFiuUqFuUqFiuUqFuUqFiuUCsqRaGmuuCsqRaGmuboCsqRaGmuuboCsqRaGmuboCsqRaGmuboCsqRaGmboCsqRaGmboCsqRaGmbobo"
-SPLIT = True
-GPI = 0
-WARM0 = 0
-WN = [512]
+HEAD = 5
+FIRST_UNITS = (1, 2, 2, 2, 2, 2, 2, 2)
+SECOND_UNITS = (2, 1, 2, 2, 1, 0, 0, 0)
+AHEAD = 8
 
 
 def tile_cfccell_pa_kernel(
@@ -214,24 +213,30 @@ def tile_cfccell_pa_kernel(
                 )
             return [(c, g2)] if u == 1 else []
 
+        def first_layer_half(h, a):
+            c = 0
+            g2, u = divmod(a, 2)
+            if (c, g2) not in ff2_rows:
+                ff2_rows[c, g2] = work.tile([P, 4, CHUNK], BF16, name="ff2_rows")
+            acc = psum.tile([P, 2, HALF], F32, name="acc", tag="bank")
+            for e in range(2):
+                for g in range(2):
+                    mx_pass(acc[:, e, :], stationary(wff2_q, a, e, g), moving(ff1_q, c, g, HALF * h, HALF), g == 0, g == 1)
+            for e in range(2):
+                nc.scalar.activation(
+                    out=ff2_rows[c, g2][:, 2 * u + e, HALF * h : HALF * (h + 1)],
+                    in_=acc[:, e, :],
+                    func=ACT.Gelu,
+                    bias=bias[:, 0, 2 * a + e : 2 * a + e + 1],
+                )
+            return [(c, g2)] if u == 1 and h == 1 else []
+
         def interleave(c, g2):
             grouped = new_grouped()
-            if GPI:
-                n = CHUNK // GPI
-                for q in range(GPI):
-                    nc.gpsimd.tensor_scalar(
-                        out=grouped[:, 4 * n * q : 4 * n * (q + 1)].rearrange("p (r t) -> p r t", t=4),
-                        in0=ff2_rows[c, g2][:, :, n * q : n * (q + 1)].rearrange("p t r -> p r t"),
-                        scalar1=1.0,
-                        scalar2=0.0,
-                        op0=ALU.mult,
-                        op1=ALU.add,
-                    )
-            else:
-                nc.vector.tensor_copy(
-                    out=grouped[:].rearrange("p (r t) -> p r t", t=4),
-                    in_=ff2_rows[c, g2][:].rearrange("p t r -> p r t"),
-                )
+            nc.vector.tensor_copy(
+                out=grouped[:].rearrange("p (r t) -> p r t", t=4),
+                in_=ff2_rows[c, g2][:].rearrange("p t r -> p r t"),
+            )
             return [(grouped[:], moving(ff2_q, c, g2))]
 
         def activate(out_tile, a, e, acc, func, bias_column, scale):
@@ -288,11 +293,11 @@ def tile_cfccell_pa_kernel(
                     )
             return gate
 
-        def subtract_state(c, a, cand):
+        def subtract_state(c, a, cand, engine=None):
             g_hx, u_hx = divmod(a, 2)
             for h in range(2):
                 hx_t = hx_grouped[c, h][:].rearrange("p (g r t) -> p g t r", g=2, t=4)
-                nc.vector.tensor_tensor(
+                (engine or nc.vector).tensor_tensor(
                     out=cand[:, h], in0=cand[:, h], in1=hx_t[:, g_hx, 2 * u_hx : 2 * u_hx + 2, :], op=ALU.subtract
                 )
 
@@ -328,72 +333,98 @@ def tile_cfccell_pa_kernel(
             )
             queue.dma_start(out=out_dram[:, first : first + 2, features], in_=out_rows[:])
 
-        st = {"pos": 0, "bl": list(range(6))}
+        raws = []
+
+        def load_next():
+            if len(raws) < len(units):
+                raws.append(units[len(raws)][0]())
+
+        for i in range(AHEAD):
+            load_next()
+            if 0 < i < 4:
+                load_bias(2 * i - 2)
+                load_bias(2 * i - 1)
+
+        prepared = []
+
+        def prepare_unit(vector_helps):
+            i = len(prepared)
+            prepared.append(i)
+            fresh = units[i][1](raws[i], vector_helps)
+            load_next()
+            return fresh
+
+        for i in range(HEAD):
+            quantise(prepare_unit(True))
+
+        bank = psum.tile([P, 2, 2, P], F32, name="bank", tag="bank")
+        nc.tensor.transpose(bank[:, 0, 0, :], bias_rows[:].bitcast(F32), ident[:])
+        bias_pairs = keep.tile([P, 2 * P], BF16, name="bias_pairs")
+        nc.vector.tensor_copy(out=bias_pairs[:].bitcast(F32), in_=bank[:, 0, 0, :])
+        bias = keep.tile([P, 6, TILES], F32, name="bias")
+        nc.vector.tensor_copy(out=bias[:].rearrange("p v j -> p (v j)"), in_=bias_pairs[:, 0 : 6 * TILES])
+        bias_gate = keep.tile([P, TILES], F32, name="bias_gate")
+        nc.vector.tensor_tensor(out=bias_gate[:], in0=bias[:, 1, :], in1=bias[:, 2, :], op=ALU.add)
+        nc.vector.tensor_scalar_mul(out=bias_gate[:], in0=bias_gate[:], scalar1=0.5)
+        bias_cand = keep.tile([P, TILES], F32, name="bias_cand")
+        nc.vector.tensor_tensor(out=bias_cand[:], in0=bias[:, 3, :], in1=bias[:, 4, :], op=ALU.add)
+
+        pairs = [(c, a) for c in range(CHUNKS) for a in range(PAIRS)]
+        for (c, a), count in zip(pairs, FIRST_UNITS):
+            done = first_layer_pair(c, a)
+            fresh = []
+            for i in range(count):
+                fresh += prepare_unit(i == 1)
+            for args in done:
+                fresh += interleave(*args)
+            quantise(fresh)
+
         fresh = []
-        rows_done = []
-        F_list = [(c, a) for c in range(CHUNKS) for a in range(PAIRS)]
-        pair_list = [(c, a) for a in range(PAIRS) for c in range(CHUNKS)]
-        lists = {k: list(pair_list) for k in "CRG"}
-        cands, recs, gates, blends = {}, {}, {}, {}
-        sub_l, add_l, mul_l, back_l, out_l = list(pair_list), list(pair_list), list(pair_list), list(pair_list), []
-        warm([CHUNK] * WARM0)
-        for token in PROGRAM:
-            if token in "uUv":
-                load, prepare = units[st["pos"]]
-                raw = load()
-                for v in st["bl"][:2]:
-                    load_bias(v)
-                st["bl"] = st["bl"][2:]
-                fresh += prepare(raw, token == "U")
-                st["pos"] += 1
-            elif token == "q":
-                quantise(fresh)
-                fresh = []
-            elif token == "i":
-                for args in rows_done:
-                    fresh += interleave(*args)
-                rows_done = []
-            elif token == "F":
-                rows_done += first_layer_pair(*F_list.pop(0))
-            elif token == "C":
-                k = lists["C"].pop(0)
-                cands[k] = input_product(*k)
-            elif token == "R":
-                k = lists["R"].pop(0)
-                recs[k] = state_product(*k)
-            elif token == "G":
-                k = lists["G"].pop(0)
-                gates[k] = gate_product_by_halves(*k) if (SPLIT and not lists["G"]) else gate_product(*k)
-            elif token == "s":
-                k = sub_l.pop(0)
-                subtract_state(k[0], k[1], cands[k])
-            elif token == "a":
-                k = add_l.pop(0)
-                add_rec(cands[k], recs[k])
-            elif token == "m":
-                k = mul_l.pop(0)
-                blends[k] = work.tile([P, 2, 2, HALF], F32, name="blend", bufs=3)
-                for h in range(2):
-                    multiply(cands[k], gates[k], blends[k], h)
-            elif token == "b":
-                k = back_l.pop(0)
-                for h in range(2):
-                    out_l.append((k[0], k[1], h, transpose_back(blends[k], h)))
-            elif token == "o":
-                for i in range(2):
-                    add_state_and_store(*out_l.pop(0), nc.gpsimd if st["pos"] < len(units) else nc.sync)
-            elif token == "w":
-                warm([CHUNK])
-            elif token == "B":
-                bank = psum.tile([P, 2, 2, P], F32, name="bank", tag="bank")
-                nc.tensor.transpose(bank[:, 0, 0, :], bias_rows[:].bitcast(F32), ident[:])
-                bias_pairs = keep.tile([P, 2 * P], BF16, name="bias_pairs")
-                nc.vector.tensor_copy(out=bias_pairs[:].bitcast(F32), in_=bank[:, 0, 0, :])
-                bias = keep.tile([P, 6, TILES], F32, name="bias")
-                nc.vector.tensor_copy(out=bias[:].rearrange("p v j -> p (v j)"), in_=bias_pairs[:, 0 : 6 * TILES])
-                bias_gate = keep.tile([P, TILES], F32, name="bias_gate")
-                nc.vector.tensor_tensor(out=bias_gate[:], in0=bias[:, 1, :], in1=bias[:, 2, :], op=ALU.add)
-                nc.vector.tensor_scalar_mul(out=bias_gate[:], in0=bias_gate[:], scalar1=0.5)
-                bias_cand = keep.tile([P, TILES], F32, name="bias_cand")
-                nc.vector.tensor_tensor(out=bias_cand[:], in0=bias[:, 3, :], in1=bias[:, 4, :], op=ALU.add)
-        assert not (fresh or rows_done or out_l or back_l or mul_l or lists["G"] or F_list) and st["pos"] == 28
+        blended = None
+        returned = None
+        pairs = [(c, a) for a in range(PAIRS) for c in range(CHUNKS)]
+        for (c, a), count in zip(pairs, SECOND_UNITS):
+            last = (c, a) == pairs[-1]
+            cand = input_product(c, a)
+            if returned is not None:
+                for back in returned:
+                    add_state_and_store(*back, nc.sync)
+            quantise(fresh)
+            rec = state_product(c, a)
+            subtract_state(c, a, cand)
+            add_rec(cand, rec)
+            gate = gate_product_by_halves(c, a) if last else gate_product(c, a)
+            if last:
+                break
+            blend = work.tile([P, 2, 2, HALF], F32, name="blend", bufs=3)
+            for h in range(2):
+                multiply(cand, gate, blend, h)
+            fresh = []
+            for i in range(count):
+                fresh += prepare_unit(False)
+            if blended is not None:
+                returned = [(blended[0], blended[1], h, transpose_back(blended[2], h)) for h in range(2)]
+            blended = (c, a, blend)
+        for h in range(2):
+            add_state_and_store(blended[0], blended[1], h, transpose_back(blended[2], h), nc.sync)
+        blend = work.tile([P, 2, 2, HALF], F32, name="blend", bufs=3)
+        for h in range(2):
+            for e in range(2):
+                nc.vector.scalar_tensor_tensor(
+                    out=blend[:, h, e, :], in0=gate[:, h, e, :], scalar=1.0, in1=cand[:, h, e, :], op0=ALU.add, op1=ALU.mult
+                )
+        banks = [transpose_back(blend, h) for h in range(2)]
+        features = slice(2 * P * a, 2 * P * (a + 1))
+        for h in range(2):
+            for n in range(2):
+                row = CHUNK_ROWS * c + 2 * h + n
+                out_last = work.tile([P, 2 * P], F32, name="out_last", bufs=4)
+                nc.vector.scalar_tensor_tensor(
+                    out=out_last[:].rearrange("b (p e) -> b p e", e=2),
+                    in0=banks[h][:, :, n, :].rearrange("b e p -> b p e"),
+                    scalar=0.5,
+                    in1=hx_nat[c, h][:, n, features].rearrange("b (p e) -> b p e", e=2),
+                    op0=ALU.mult,
+                    op1=ALU.add,
+                )
+                nc.sync.dma_start(out=out_dram[:, row, features], in_=out_last[:])

@@ -27,9 +27,9 @@ TILES = 2 * PAIRS
 UNIT = 2048
 UNIT_COLS = UNIT // 4
 
-HEAD = 5
-FIRST_UNITS = (1, 2, 2, 2, 2, 2, 2, 2)
-SECOND_UNITS = (2, 1, 2, 2, 1, 0, 0, 0)
+HEAD = 3
+FIRST_UNITS = (2, 2, 2, 2, 2, 2, 2, 2)
+SECOND_UNITS = (2, 2, 2, 2, 1, 0, 0, 0)
 AHEAD = 8
 
 
@@ -355,7 +355,7 @@ def tile_cfccell_pa_kernel(
             return fresh
 
         for i in range(HEAD):
-            quantise(prepare_unit(True))
+            quantise(prepare_unit(i == 0))
 
         bank = psum.tile([P, 2, 2, P], F32, name="bank", tag="bank")
         nc.tensor.transpose(bank[:, 0, 0, :], bias_rows[:].bitcast(F32), ident[:])
@@ -369,44 +369,47 @@ def tile_cfccell_pa_kernel(
         bias_cand = keep.tile([P, TILES], F32, name="bias_cand")
         nc.vector.tensor_tensor(out=bias_cand[:], in0=bias[:, 3, :], in1=bias[:, 4, :], op=ALU.add)
 
+        fresh = []
         pairs = [(c, a) for c in range(CHUNKS) for a in range(PAIRS)]
         for (c, a), count in zip(pairs, FIRST_UNITS):
-            done = first_layer_pair(c, a)
-            fresh = []
             for i in range(count):
                 fresh += prepare_unit(i == 1)
-            for args in done:
-                fresh += interleave(*args)
             quantise(fresh)
+            fresh = []
+            for args in first_layer_pair(c, a):
+                fresh += interleave(*args)
 
-        fresh = []
         blended = None
-        returned = None
+        returned = []
         pairs = [(c, a) for a in range(PAIRS) for c in range(CHUNKS)]
-        for (c, a), count in zip(pairs, SECOND_UNITS):
-            last = (c, a) == pairs[-1]
-            cand = input_product(c, a)
-            if returned is not None:
-                for back in returned:
-                    add_state_and_store(*back, nc.sync)
+        cands = [input_product(*pairs[0])]
+        for k, count in enumerate(SECOND_UNITS):
+            c, a = pairs[k]
+            last = k == len(pairs) - 1
+            cand = cands[k]
             quantise(fresh)
             rec = state_product(c, a)
+            for back in returned:
+                add_state_and_store(*back, nc.sync)
             subtract_state(c, a, cand)
             add_rec(cand, rec)
-            gate = gate_product_by_halves(c, a) if last else gate_product(c, a)
             if last:
+                gate = gate_product_by_halves(c, a)
+                returned = [(blended[0], blended[1], h, transpose_back(blended[2], h)) for h in range(2)]
                 break
-            blend = work.tile([P, 2, 2, HALF], F32, name="blend", bufs=3)
-            for h in range(2):
-                multiply(cand, gate, blend, h)
+            gate = gate_product(c, a)
             fresh = []
             for i in range(count):
                 fresh += prepare_unit(False)
+            blend = work.tile([P, 2, 2, HALF], F32, name="blend", bufs=3)
+            for h in range(2):
+                multiply(cand, gate, blend, h)
             if blended is not None:
                 returned = [(blended[0], blended[1], h, transpose_back(blended[2], h)) for h in range(2)]
             blended = (c, a, blend)
-        for h in range(2):
-            add_state_and_store(blended[0], blended[1], h, transpose_back(blended[2], h), nc.sync)
+            cands.append(input_product(*pairs[k + 1]))
+        for back in returned:
+            add_state_and_store(*back, nc.sync)
         blend = work.tile([P, 2, 2, HALF], F32, name="blend", bufs=3)
         for h in range(2):
             for e in range(2):

@@ -68,24 +68,25 @@ def tile_cfccell_pa_kernel(
                 in_=vectors[v].rearrange("(a w) -> a w", a=PAIRS),
             )
 
-        def mx_operand(name, width):
-            codes = keep.tile([P, width], U32, name=name + "_codes", align_bytes=64)
-            scales = keep.tile([P, width], U8, name=name + "_scales", align_bytes=64)
-            return codes, scales
+        def mx_operand(name, width, weights):
+            code_start, scale_start = (128, 64) if weights else (0, 192)
+            codes = keep.tile([P, width + code_start // 4], U32, name=name + "_codes", align_bytes=256)
+            scales = keep.tile([P, width + scale_start], U8, name=name + "_scales", align_bytes=256)
+            return codes[:, code_start // 4 :], scales[:, scale_start:]
 
         def columns(operand, first, count):
             codes, scales = operand
             return codes[:, first : first + count], scales[:, first : first + count]
 
-        ff1_q = mx_operand("ff1", 2 * BATCH)
-        hx_q = mx_operand("hx", 2 * BATCH)
-        ff2_q = mx_operand("ff2", 2 * BATCH)
-        x_q = mx_operand("x", BATCH)
-        wff2_q = mx_operand("wff2", 2 * HIDDEN)
-        wta_q = mx_operand("wta", 2 * HIDDEN)
-        wtb_q = mx_operand("wtb", 2 * HIDDEN)
-        wr_q = mx_operand("wr", 2 * HIDDEN)
-        win_q = mx_operand("win", HIDDEN)
+        ff1_q = mx_operand("ff1", 2 * BATCH, False)
+        hx_q = mx_operand("hx", 2 * BATCH, False)
+        ff2_q = mx_operand("ff2", 2 * BATCH, False)
+        x_q = mx_operand("x", BATCH, False)
+        wff2_q = mx_operand("wff2", 2 * HIDDEN, True)
+        wta_q = mx_operand("wta", 2 * HIDDEN, True)
+        wtb_q = mx_operand("wtb", 2 * HIDDEN, True)
+        wr_q = mx_operand("wr", 2 * HIDDEN, True)
+        win_q = mx_operand("win", HIDDEN, True)
 
         def moving(operand, c, g, first=0, count=CHUNK):
             return columns(operand, BATCH * g + CHUNK * c + first, count)

@@ -40,7 +40,7 @@ def tile_cfccell_pa_kernel(
     with ExitStack() as ctx:
         keep = ctx.enter_context(tc.tile_pool(name="keep", bufs=1))
         stream = ctx.enter_context(tc.tile_pool(name="stream", bufs=8))
-        stage = ctx.enter_context(tc.tile_pool(name="stage", bufs=6))
+        stage = ctx.enter_context(tc.tile_pool(name="stage", bufs=5))
         work = ctx.enter_context(tc.tile_pool(name="work", bufs=2))
         psum = ctx.enter_context(tc.psum_pool(name="psum", bufs=8))
         ctx.enter_context(tc.manual_schedule())
@@ -49,6 +49,8 @@ def tile_cfccell_pa_kernel(
         nc.vector.memset(warm_in[:], 0.0)
         ident = keep.tile([P, P], F32, name="ident")
         make_identity(nc, ident[:])
+        twice = keep.tile([P, P], BF16, name="twice")
+        nc.vector.tensor_scalar(out=twice[:], in0=ident[:], scalar1=2.0, scalar2=None, op0=ALU.mult)
         table = keep.tile([P, 1], F32, name="table")
         nc.vector.memset(table[:], 0.0)
         nc.scalar.activation(out=table[:], in_=table[:], func=ACT.Gelu)
@@ -320,6 +322,43 @@ def tile_cfccell_pa_kernel(
                     nc.tensor.transpose(bank[:, e, n, :], blend[:, half, e, P * n : P * (n + 1)], ident[:])
             return bank
 
+        def state_bank(c, a, half):
+            features = slice(2 * P * a, 2 * P * (a + 1))
+            bank = psum.tile([P, 2, 2, P], F32, name="bank", tag="bank")
+            nc.tensor.matmul(
+                bank[:],
+                lhsT=twice[:],
+                rhs=hx_nat[c, half][:, :, features].rearrange("b n (p e) -> b e n p", e=2),
+                start=True,
+                stop=False,
+            )
+            return bank
+
+        def add_transposed(bank, blend, half):
+            for e in range(2):
+                for n in range(2):
+                    nc.tensor.matmul(
+                        bank[:, e, n, :],
+                        lhsT=blend[:, half, e, P * n : P * (n + 1)],
+                        rhs=ident[:],
+                        is_transpose=True,
+                        start=False,
+                        stop=e == 1 and n == 1,
+                    )
+
+        def halve_and_store(c, a, half, bank, on_vector):
+            features = slice(2 * P * a, 2 * P * (a + 1))
+            first = CHUNK_ROWS * c + 2 * half
+            for n in range(2):
+                out_last = work.tile([P, 2 * P], F32, name="out_last", bufs=8)
+                target = out_last[:].rearrange("b (p e) -> b p e", e=2)
+                source = bank[:, :, n, :].rearrange("b e p -> b p e")
+                if on_vector:
+                    nc.vector.tensor_scalar_mul(out=target, in0=source, scalar1=0.5)
+                else:
+                    nc.scalar.mul(target, source, 0.5)
+                nc.sync.dma_start(out=out_dram[:, first + n, features], in_=out_last[:])
+
         def add_state_and_store(c, a, half, bank, queue):
             features = slice(2 * P * a, 2 * P * (a + 1))
             first = CHUNK_ROWS * c + 2 * half
@@ -396,7 +435,6 @@ def tile_cfccell_pa_kernel(
             add_rec(cand, rec)
             if last:
                 gate = gate_product_by_halves(c, a)
-                returned = [(blended[0], blended[1], h, transpose_back(blended[2], h)) for h in range(2)]
                 break
             gate = gate_product(c, a)
             fresh = []
@@ -409,26 +447,17 @@ def tile_cfccell_pa_kernel(
                 returned = [(blended[0], blended[1], h, transpose_back(blended[2], h)) for h in range(2)]
             blended = (c, a, blend)
             cands.append(input_product(*pairs[k + 1]))
-        for back in returned:
-            add_state_and_store(*back, nc.sync)
+        banks = [state_bank(blended[0], blended[1], h) for h in range(2)]
+        for h in range(2):
+            add_transposed(banks[h], blended[2], h)
+            halve_and_store(blended[0], blended[1], h, banks[h], False)
+        banks = [state_bank(c, a, h) for h in range(2)]
         blend = work.tile([P, 2, 2, HALF], F32, name="blend", bufs=3)
         for h in range(2):
             for e in range(2):
                 nc.vector.scalar_tensor_tensor(
                     out=blend[:, h, e, :], in0=gate[:, h, e, :], scalar=1.0, in1=cand[:, h, e, :], op0=ALU.add, op1=ALU.mult
                 )
-        banks = [transpose_back(blend, h) for h in range(2)]
-        features = slice(2 * P * a, 2 * P * (a + 1))
         for h in range(2):
-            for n in range(2):
-                row = CHUNK_ROWS * c + 2 * h + n
-                out_last = work.tile([P, 2 * P], F32, name="out_last", bufs=4)
-                nc.vector.scalar_tensor_tensor(
-                    out=out_last[:].rearrange("b (p e) -> b p e", e=2),
-                    in0=banks[h][:, :, n, :].rearrange("b e p -> b p e"),
-                    scalar=0.5,
-                    in1=hx_nat[c, h][:, n, features].rearrange("b (p e) -> b p e", e=2),
-                    op0=ALU.mult,
-                    op1=ALU.add,
-                )
-                nc.sync.dma_start(out=out_dram[:, row, features], in_=out_last[:])
+            add_transposed(banks[h], blend, h)
+            halve_and_store(c, a, h, banks[h], h == 1)

@@ -237,8 +237,8 @@ def tile_cfccell_pa_kernel(
         def interleave(c, g2):
             grouped = new_grouped()
             nc.vector.tensor_copy(
-                out=grouped[:].rearrange("p (r t) -> p r t", t=4),
-                in_=ff2_rows[c, g2][:].rearrange("p t r -> p r t"),
+                out=grouped[:].rearrange("p (s i t) -> p s t i", i=4, t=4),
+                in_=ff2_rows[c, g2][:].rearrange("p t (s i) -> p s t i", i=4),
             )
             return [(grouped[:], moving(ff2_q, c, g2))]
 

@@ -362,16 +362,16 @@ def tile_cfccell_pa_kernel(
         def add_state_and_store(c, a, half, bank, queue):
             features = slice(2 * P * a, 2 * P * (a + 1))
             first = CHUNK_ROWS * c + 2 * half
-            out_rows = work.tile([P, 2, 2 * P], F32, name="out_rows", bufs=4)
+            out_rows = spare.pop(0)
             nc.vector.scalar_tensor_tensor(
-                out=out_rows[:].rearrange("b n (p e) -> b n p e", e=2),
+                out=out_rows.rearrange("b n (p e) -> b n p e", e=2),
                 in0=bank[:].rearrange("b e n p -> b n p e"),
                 scalar=0.5,
                 in1=hx_nat[c, half][:, :, features].rearrange("b n (p e) -> b n p e", e=2),
                 op0=ALU.mult,
                 op1=ALU.add,
             )
-            queue.dma_start(out=out_dram[:, first : first + 2, features], in_=out_rows[:])
+            queue.dma_start(out=out_dram[:, first : first + 2, features], in_=out_rows)
 
         raws = []
 
@@ -399,15 +399,15 @@ def tile_cfccell_pa_kernel(
 
         bank = psum.tile([P, 2, 2, P], F32, name="bank", tag="bank")
         nc.tensor.transpose(bank[:, 0, 0, :], bias_rows[:].bitcast(F32), ident[:])
-        bias_pairs = keep.tile([P, 2 * P], BF16, name="bias_pairs")
-        nc.vector.tensor_copy(out=bias_pairs[:].bitcast(F32), in_=bank[:, 0, 0, :])
         bias = keep.tile([P, 6, TILES], F32, name="bias")
-        nc.vector.tensor_copy(out=bias[:].rearrange("p v j -> p (v j)"), in_=bias_pairs[:, 0 : 6 * TILES])
+        nc.vector.tensor_copy(
+            out=bias[:].rearrange("p v j -> p (v j)"), in_=bank[:, 0, 0, 0 : 3 * TILES].bitcast(BF16)
+        )
         bias_gate = keep.tile([P, TILES], F32, name="bias_gate")
         nc.vector.tensor_tensor(out=bias_gate[:], in0=bias[:, 1, :], in1=bias[:, 2, :], op=ALU.add)
-        nc.vector.tensor_scalar_mul(out=bias_gate[:], in0=bias_gate[:], scalar1=0.5)
         bias_cand = keep.tile([P, TILES], F32, name="bias_cand")
         nc.vector.tensor_tensor(out=bias_cand[:], in0=bias[:, 3, :], in1=bias[:, 4, :], op=ALU.add)
+        nc.vector.tensor_scalar(out=bias_gate[:], in0=bias_gate[:], scalar1=0.5, scalar2=None, op0=ALU.mult)
 
         fresh = []
         pairs = [(c, a) for c in range(CHUNKS) for a in range(PAIRS)]
@@ -419,6 +419,14 @@ def tile_cfccell_pa_kernel(
             for args in first_layer_pair(c, a):
                 fresh += interleave(*args)
 
+        spare = []
+        for name in ("ff1", "wff2"):
+            block = keep.tile([P, 4, 2, 2 * P], F32, name=name + "_codes", align_bytes=256)
+            spare += [block[:, i] for i in range(4)]
+        for i in range(4):
+            out_rows = work.tile([P, 2, 2 * P], F32, name="out_rows", bufs=4)
+            spare.append(out_rows[:])
+
         blended = None
         returned = []
         pairs = [(c, a) for a in range(PAIRS) for c in range(CHUNKS)]
@@ -427,10 +435,10 @@ def tile_cfccell_pa_kernel(
             c, a = pairs[k]
             last = k == len(pairs) - 1
             cand = cands[k]
-            quantise(fresh)
-            rec = state_product(c, a)
             for back in returned:
                 add_state_and_store(*back, nc.sync)
+            quantise(fresh)
+            rec = state_product(c, a)
             subtract_state(c, a, cand)
             add_rec(cand, rec)
             if last:

@@ -45,23 +45,15 @@ def tile_cfccell_pa_kernel(
         psum = ctx.enter_context(tc.psum_pool(name="psum", bufs=8))
         ctx.enter_context(tc.manual_schedule())
 
-        warm_in = keep.tile([P, CHUNK], BF16, name="warm_in")
-        nc.vector.memset(warm_in[:], 0.0)
-        ident = keep.tile([P, P], F32, name="ident")
-        make_identity(nc, ident[:])
-        twice = keep.tile([P, P], BF16, name="twice")
-        nc.vector.tensor_scalar(out=twice[:], in0=ident[:], scalar1=2.0, scalar2=None, op0=ALU.mult)
         table = keep.tile([P, 1], F32, name="table")
         nc.vector.memset(table[:], 0.0)
         nc.scalar.activation(out=table[:], in_=table[:], func=ACT.Gelu)
-
-        def warm(sizes):
-            for n in sizes:
-                bank = psum.tile([P, CHUNK], F32, name="idle", tag="bank")
-                nc.tensor.matmul(bank[:, 0:n], lhsT=warm_in[:, 0:P], rhs=warm_in[:, 0:n], start=True, stop=True)
-
         bias_rows = keep.tile([P, 2 * P], BF16, name="bias_rows")
         nc.vector.memset(bias_rows[:], 0.0)
+        ident = keep.tile([P, P], F32, name="ident")
+        make_identity(nc, ident[:])
+        twice = keep.tile([P, P], BF16, name="twice")
+        nc.gpsimd.tensor_scalar(out=twice[:], in0=ident[:], scalar1=2.0, scalar2=None, op0=ALU.mult)
         vectors = [b_ff2, b_ta, b_tb, b_in, input_b, r_b]
 
         def load_bias(v):
@@ -404,10 +396,10 @@ def tile_cfccell_pa_kernel(
             out=bias[:].rearrange("p v j -> p (v j)"), in_=bank[:, 0, 0, 0 : 3 * TILES].bitcast(BF16)
         )
         bias_gate = keep.tile([P, TILES], F32, name="bias_gate")
-        nc.vector.tensor_tensor(out=bias_gate[:], in0=bias[:, 1, :], in1=bias[:, 2, :], op=ALU.add)
+        nc.gpsimd.tensor_tensor(out=bias_gate[:], in0=bias[:, 1, :], in1=bias[:, 2, :], op=ALU.add)
         bias_cand = keep.tile([P, TILES], F32, name="bias_cand")
-        nc.vector.tensor_tensor(out=bias_cand[:], in0=bias[:, 3, :], in1=bias[:, 4, :], op=ALU.add)
-        nc.vector.tensor_scalar(out=bias_gate[:], in0=bias_gate[:], scalar1=0.5, scalar2=None, op0=ALU.mult)
+        nc.gpsimd.tensor_tensor(out=bias_cand[:], in0=bias[:, 3, :], in1=bias[:, 4, :], op=ALU.add)
+        nc.gpsimd.tensor_scalar(out=bias_gate[:], in0=bias_gate[:], scalar1=0.5, scalar2=None, op0=ALU.mult)
 
         fresh = []
         pairs = [(c, a) for c in range(CHUNKS) for a in range(PAIRS)]

@@ -271,17 +271,22 @@ def tile_cfccell_pa_kernel(
                 activate(gate, a, e, acc, ACT.Tanh, bias_gate, 0.5)
             return gate
 
+        def last_pieces():
+            pieces = [(h, e, 0, HALF) for h in range(2) for e in range(2)]
+            return pieces
+
         def gate_product_by_halves(c, a):
             gate = work.tile([P, 2, 2, HALF], F32, name="gate")
-            for h in range(2):
+            for half in range(2):
                 acc = psum.tile([P, 2, HALF], F32, name="acc", tag="bank")
-                for e in range(2):
+                pieces = [(e, lo, n) for h, e, lo, n in last_pieces() if h == half]
+                for e, lo, n in pieces:
                     for i, (w_q, g) in enumerate(gate_terms):
-                        mx_pass(acc[:, e, :], stationary(w_q, a, e, g), moving(ff2_q, c, g, HALF * h, HALF), i == 0, i == 3)
-                for e in range(2):
+                        mx_pass(acc[:, e, lo : lo + n], stationary(w_q, a, e, g), moving(ff2_q, c, g, HALF * half + lo, n), i == 0, i == 3)
+                for e, lo, n in pieces:
                     nc.scalar.activation(
-                        out=gate[:, h, e, :],
-                        in_=acc[:, e, :],
+                        out=gate[:, half, e, lo : lo + n],
+                        in_=acc[:, e, lo : lo + n],
                         func=ACT.Tanh,
                         bias=bias_gate[:, 2 * a + e : 2 * a + e + 1],
                         scale=0.5,
@@ -337,6 +342,49 @@ def tile_cfccell_pa_kernel(
                         start=False,
                         stop=e == 1 and n == 1,
                     )
+
+        def finish_by_tiles(c, a, cand, gate):
+            features = slice(2 * P * a, 2 * P * (a + 1))
+            banks = []
+            for n in range(CHUNK_ROWS):
+                bank = psum.tile([P, 2, P], F32, name="bank", tag="bank")
+                nc.tensor.matmul(
+                    bank[:],
+                    lhsT=twice[:],
+                    rhs=hx_nat[c, n // HALF_ROWS][:, n % HALF_ROWS, features].rearrange("b (p e) -> b e p", e=2),
+                    start=True,
+                    stop=False,
+                )
+                banks.append(bank)
+            blend = work.tile([P, 2, 2, HALF], F32, name="blend", bufs=3)
+            for h, e, lo, n in last_pieces():
+                nc.vector.scalar_tensor_tensor(
+                    out=blend[:, h, e, lo : lo + n],
+                    in0=gate[:, h, e, lo : lo + n],
+                    scalar=1.0,
+                    in1=cand[:, h, e, lo : lo + n],
+                    op0=ALU.add,
+                    op1=ALU.mult,
+                )
+            for n in range(CHUNK_ROWS):
+                h, first = n // HALF_ROWS, P * (n % HALF_ROWS)
+                for e in range(2):
+                    nc.tensor.matmul(
+                        banks[n][:, e, :],
+                        lhsT=blend[:, h, e, first : first + P],
+                        rhs=ident[:],
+                        is_transpose=True,
+                        start=False,
+                        stop=e == 1,
+                    )
+                out_last = work.tile([P, 2 * P], F32, name="out_last", bufs=8)
+                target = out_last[:].rearrange("b (p e) -> b p e", e=2)
+                source = banks[n][:].rearrange("b e p -> b p e")
+                if n % 2 == 0:
+                    nc.scalar.mul(target, source, 0.5)
+                else:
+                    nc.vector.tensor_scalar_mul(out=target, in0=source, scalar1=0.5)
+                nc.sync.dma_start(out=out_dram[:, CHUNK_ROWS * c + n, features], in_=out_last[:])
 
         def halve_and_store(c, a, half, bank, on_vector):
             features = slice(2 * P * a, 2 * P * (a + 1))
@@ -405,7 +453,7 @@ def tile_cfccell_pa_kernel(
         pairs = [(c, a) for c in range(CHUNKS) for a in range(PAIRS)]
         for (c, a), count in zip(pairs, FIRST_UNITS):
             for i in range(count):
-                fresh += prepare_unit(i == 1)
+                fresh += prepare_unit(i == 1 or (c, a) == (0, 1))
             quantise(fresh)
             fresh = []
             for args in first_layer_pair(c, a):
@@ -451,13 +499,4 @@ def tile_cfccell_pa_kernel(
         for h in range(2):
             add_transposed(banks[h], blended[2], h)
             halve_and_store(blended[0], blended[1], h, banks[h], False)
-        banks = [state_bank(c, a, h) for h in range(2)]
-        blend = work.tile([P, 2, 2, HALF], F32, name="blend", bufs=3)
-        for h in range(2):
-            for e in range(2):
-                nc.vector.scalar_tensor_tensor(
-                    out=blend[:, h, e, :], in0=gate[:, h, e, :], scalar=1.0, in1=cand[:, h, e, :], op0=ALU.add, op1=ALU.mult
-                )
-        for h in range(2):
-            add_transposed(banks[h], blend, h)
-            halve_and_store(c, a, h, banks[h], h == 1)
+        finish_by_tiles(c, a, cand, gate)

from contextlib import ExitStack

import concourse.mybir as mybir
from concourse.masks import make_identity

F32 = mybir.dt.float32
BF16 = mybir.dt.bfloat16
U32 = mybir.dt.uint32
U8 = mybir.dt.uint8
FP8X4 = mybir.dt.float8_e4m3fn_x4
ACT = mybir.ActivationFunctionType
ALU = mybir.AluOpType

P = 128
BATCH, IN_FEATURES, HIDDEN = 1024, 512, 1024
FLOPS = 2 * BATCH * HIDDEN * (4 * HIDDEN + IN_FEATURES)

K_PASS = 512
CHUNK = 512
CHUNKS = BATCH // CHUNK
HALF = CHUNK // 2
ROWS = BATCH // P
CHUNK_ROWS = CHUNK // P
HALF_ROWS = HALF // P
PAIRS = HIDDEN // (2 * P)
TILES = 2 * PAIRS
UNIT = 2048
UNIT_COLS = UNIT // 4

HEAD = 3
FIRST_UNITS = (2, 2, 2, 2, 2, 2, 2, 2)
SECOND_UNITS = (2, 2, 2, 2, 1, 0, 0, 0)
AHEAD = 8


def tile_cfccell_pa_kernel(
    tc, ff1, x, hx, W_ff2, b_ff2, W_ta, b_ta, W_tb, b_tb, W_in, b_in, input_b, W_r, r_b, out
):
    nc = tc.nc
    with ExitStack() as ctx:
        keep = ctx.enter_context(tc.tile_pool(name="keep", bufs=1))
        stream = ctx.enter_context(tc.tile_pool(name="stream", bufs=8))
        stage = ctx.enter_context(tc.tile_pool(name="stage", bufs=5))
        work = ctx.enter_context(tc.tile_pool(name="work", bufs=2))
        psum = ctx.enter_context(tc.psum_pool(name="psum", bufs=8))
        ctx.enter_context(tc.manual_schedule())

        table = keep.tile([P, 1], F32, name="table")
        nc.vector.memset(table[:], 0.0)
        nc.scalar.activation(out=table[:], in_=table[:], func=ACT.Gelu)
        bias_rows = keep.tile([P, 2 * P], BF16, name="bias_rows")
        nc.vector.memset(bias_rows[:], 0.0)
        ident = keep.tile([P, P], F32, name="ident")
        make_identity(nc, ident[:])
        twice = keep.tile([P, P], BF16, name="twice")
        nc.gpsimd.tensor_scalar(out=twice[:], in0=ident[:], scalar1=2.0, scalar2=None, op0=ALU.mult)
        vectors = [b_ff2, b_ta, b_tb, b_in, input_b, r_b]

        def load_bias(v):
            nc.sync.dma_start(
                out=bias_rows[PAIRS * v : PAIRS * (v + 1), :],
                in_=vectors[v].rearrange("(a w) -> a w", a=PAIRS),
            )

        def mx_operand(name, width, weights):
            code_start, scale_start = (128, 64) if weights else (0, 192)
            codes = keep.tile([P, width + code_start // 4], U32, name=name + "_codes", align_bytes=256)
            scales = keep.tile([P, width + scale_start], U8, name=name + "_scales", align_bytes=256)
            return codes[:, code_start // 4 :], scales[:, scale_start:]

        def columns(operand, first, count):
            codes, scales = operand
            return codes[:, first : first + count], scales[:, first : first + count]

        ff1_q = mx_operand("ff1", 2 * BATCH, False)
        hx_q = mx_operand("hx", 2 * BATCH, False)
        ff2_q = mx_operand("ff2", 2 * BATCH, False)
        x_q = mx_operand("x", BATCH, False)
        wff2_q = mx_operand("wff2", 2 * HIDDEN, True)
        wta_q = mx_operand("wta", 2 * HIDDEN, True)
        wtb_q = mx_operand("wtb", 2 * HIDDEN, True)
        wr_q = mx_operand("wr", 2 * HIDDEN, True)
        win_q = mx_operand("win", HIDDEN, True)

        def moving(operand, c, g, first=0, count=CHUNK):
            return columns(operand, BATCH * g + CHUNK * c + first, count)

        def stationary(operand, a, e, g):
            return columns(operand, UNIT_COLS * a + P * (2 * e + g), P)

        def mx_pass(acc, weights, acts, start, stop):
            nc.tensor.matmul_mx(
                out=acc,
                lhsT=weights[0].bitcast(FP8X4),
                lhsT_scale=weights[1],
                rhs=acts[0].bitcast(FP8X4),
                rhs_scale=acts[1],
                start=start,
                stop=stop,
            )

        def transpose_unit(blocks, grouped, vector_helps):
            words = grouped[:].bitcast(F32).rearrange("p (b r u) -> p b r u", b=4, u=2)
            for half in range(2):
                bank = psum.tile([P, 2, 2, P], F32, name="bank", tag="bank")
                for b in range(2):
                    for u in range(2):
                        nc.tensor.transpose(bank[:, b, u, :], blocks[2 * half + b][:, u, :], ident[:])
                copy_out = nc.vector.tensor_copy if vector_helps and half == 1 else nc.scalar.copy
                copy_out(
                    out=words[:, 2 * half : 2 * half + 2, :, :],
                    in_=bank[:].rearrange("p b u r -> p b r u"),
                )

        def quantise(ready):
            for source, (codes, scales) in ready:
                nc.vector.quantize_mx(out=codes.bitcast(FP8X4), scales=scales, in_=source)

        def new_grouped():
            return stage.tile([P, UNIT], BF16, name="grouped", align_bytes=64)

        def weight_unit(pieces, dest):
            def load():
                raw = stream.tile([P, 4, K_PASS], BF16, name="raw")
                first = 0
                for piece in pieces:
                    nc.sync.dma_start(out=raw[:, first : first + piece.shape[1], :], in_=piece)
                    first += piece.shape[1]
                return raw

            def prepare(raw, vector_helps):
                grouped = new_grouped()
                words = raw[:].rearrange("p b k -> p (b k)").bitcast(F32).rearrange("p (b u w) -> p b u w", b=4, u=2)
                transpose_unit([words[:, b] for b in range(4)], grouped, vector_helps)
                return [(grouped[:], dest)]

            return load, prepare

        def pair_weights(source, operand, a, cut=1):
            rows = source.rearrange("(a p e) k -> a p (e k)", p=P, e=2)[a].rearrange("p (b k) -> p b k", b=4)
            n = 4 // cut
            return weight_unit([rows[:, n * i : n * (i + 1)] for i in range(cut)], columns(operand, UNIT_COLS * a, UNIT_COLS))

        def input_weights(h):
            rows = W_in.rearrange("(a p e) k -> a p e k", p=P, e=2)
            return weight_unit([rows[2 * h], rows[2 * h + 1]], columns(win_q, UNIT_COLS * h, UNIT_COLS))

        def input_rows(c):
            rows = x.rearrange("(p n) k -> p n k", n=ROWS)[:, CHUNK_ROWS * c : CHUNK_ROWS * (c + 1), :]
            return weight_unit([rows], moving(x_q, c, 0))

        def half_chunk(source, operand, c, h, tiles, kept):
            first = CHUNK_ROWS * c + HALF_ROWS * h

            def load():
                raw = tiles()
                nc.sync.dma_start(out=raw[:], in_=source.rearrange("(p n) k -> p n k", n=ROWS)[:, first : first + HALF_ROWS, :])
                return raw

            def prepare(raw, vector_helps):
                grouped = kept if kept is not None else new_grouped()
                words = raw[:].rearrange("p n k -> p (n k)").bitcast(F32).rearrange("p (n g u w) -> p g n u w", n=HALF_ROWS, g=2, u=2)
                transpose_unit([words[:, g, n] for g in range(2) for n in range(HALF_ROWS)], grouped, vector_helps)
                return [
                    (grouped[:, 4 * HALF * g : 4 * HALF * (g + 1)], moving(operand, c, g, HALF * h, HALF))
                    for g in range(2)
                ]

            return load, prepare

        hx_nat = {}
        hx_grouped = {}

        def backbone_half(c, h):
            return half_chunk(ff1, ff1_q, c, h, lambda: stream.tile([P, HALF_ROWS, HIDDEN], BF16, name="raw"), None)

        def state_half(c, h):
            hx_nat[c, h] = keep.tile([P, HALF_ROWS, HIDDEN], BF16, name="hx_nat_%d_%d" % (c, h))
            hx_grouped[c, h] = keep.tile([P, UNIT], BF16, name="hx_grouped_%d_%d" % (c, h), align_bytes=64)
            return half_chunk(hx, hx_q, c, h, lambda: hx_nat[c, h], hx_grouped[c, h])

        units = [pair_weights(W_ff2, wff2_q, 0, 2)]
        units += [backbone_half(0, h) for h in range(2)]
        units += [pair_weights(W_ff2, wff2_q, a) for a in range(1, PAIRS)]
        units += [backbone_half(1, h) for h in range(2)]
        units += [input_rows(c) for c in range(CHUNKS)]
        units += [state_half(c, h) for c in range(CHUNKS) for h in range(2)]
        for a in range(PAIRS):
            if a % 2 == 0:
                units.append(input_weights(a // 2))
            units += [pair_weights(W_r, wr_q, a), pair_weights(W_ta, wta_q, a), pair_weights(W_tb, wtb_q, a)]

        ff2_rows = {}

        def first_layer_pair(c, a):
            g2, u = divmod(a, 2)
            if u == 0:
                ff2_rows[c, g2] = work.tile([P, 4, CHUNK], BF16, name="ff2_rows")
            for e in range(2):
                acc = psum.tile([P, CHUNK], F32, name="acc", tag="bank")
                for g in range(2):
                    mx_pass(acc[:], stationary(wff2_q, a, e, g), moving(ff1_q, c, g), g == 0, g == 1)
                nc.scalar.activation(
                    out=ff2_rows[c, g2][:, 2 * u + e, :],
                    in_=acc[:],
                    func=ACT.Gelu,
                    bias=bias[:, 0, 2 * a + e : 2 * a + e + 1],
                )
            return [(c, g2)] if u == 1 else []

        def first_layer_half(h, a):
            c = 0
            g2, u = divmod(a, 2)
            if (c, g2) not in ff2_rows:
                ff2_rows[c, g2] = work.tile([P, 4, CHUNK], BF16, name="ff2_rows")
            acc = psum.tile([P, 2, HALF], F32, name="acc", tag="bank")
            for e in range(2):
                for g in range(2):
                    mx_pass(acc[:, e, :], stationary(wff2_q, a, e, g), moving(ff1_q, c, g, HALF * h, HALF), g == 0, g == 1)
            for e in range(2):
                nc.scalar.activation(
                    out=ff2_rows[c, g2][:, 2 * u + e, HALF * h : HALF * (h + 1)],
                    in_=acc[:, e, :],
                    func=ACT.Gelu,
                    bias=bias[:, 0, 2 * a + e : 2 * a + e + 1],
                )
            return [(c, g2)] if u == 1 and h == 1 else []

        def interleave(c, g2):
            grouped = new_grouped()
            nc.vector.tensor_copy(
                out=grouped[:].rearrange("p (s i t) -> p s t i", i=4, t=4),
                in_=ff2_rows[c, g2][:].rearrange("p t (s i) -> p s t i", i=4),
            )
            return [(grouped[:], moving(ff2_q, c, g2))]

        def activate(out_tile, a, e, acc, func, bias_column, scale):
            nc.scalar.activation(
                out=out_tile[:, :, e, :],
                in_=acc[:].rearrange("p (h r) -> p h r", h=2),
                func=func,
                bias=bias_column[:, 2 * a + e : 2 * a + e + 1],
                scale=scale,
            )

        def input_product(c, a):
            cand = work.tile([P, 2, 2, HALF], F32, name="cand", bufs=3)
            for e in range(2):
                acc = psum.tile([P, CHUNK], F32, name="acc", tag="bank")
                mx_pass(acc[:], columns(win_q, P * (2 * a + e), P), moving(x_q, c, 0), True, True)
                activate(cand, a, e, acc, ACT.Gelu, bias_cand, 1.0)
            return cand

        def state_product(c, a):
            rec = work.tile([P, 2, 2, HALF], F32, name="rec")
            for e in range(2):
                acc = psum.tile([P, CHUNK], F32, name="acc", tag="bank")
                for g in range(2):
                    mx_pass(acc[:], stationary(wr_q, a, e, g), moving(hx_q, c, g), g == 0, g == 1)
                activate(rec, a, e, acc, ACT.Gelu, bias[:, 5, :], 1.0)
            return rec

        gate_terms = [(wta_q, 0), (wta_q, 1), (wtb_q, 0), (wtb_q, 1)]

        def gate_product(c, a):
            gate = work.tile([P, 2, 2, HALF], F32, name="gate")
            for e in range(2):
                acc = psum.tile([P, CHUNK], F32, name="acc", tag="bank")
                for i, (w_q, g) in enumerate(gate_terms):
                    mx_pass(acc[:], stationary(w_q, a, e, g), moving(ff2_q, c, g), i == 0, i == 3)
                activate(gate, a, e, acc, ACT.Tanh, bias_gate, 0.5)
            return gate

        def last_pieces():
            pieces = [(h, e, 0, HALF) for h in range(2) for e in range(2)]
            return pieces

        def gate_product_by_halves(c, a):
            gate = work.tile([P, 2, 2, HALF], F32, name="gate")
            for half in range(2):
                acc = psum.tile([P, 2, HALF], F32, name="acc", tag="bank")
                pieces = [(e, lo, n) for h, e, lo, n in last_pieces() if h == half]
                for e, lo, n in pieces:
                    for i, (w_q, g) in enumerate(gate_terms):
                        mx_pass(acc[:, e, lo : lo + n], stationary(w_q, a, e, g), moving(ff2_q, c, g, HALF * half + lo, n), i == 0, i == 3)
                for e, lo, n in pieces:
                    nc.scalar.activation(
                        out=gate[:, half, e, lo : lo + n],
                        in_=acc[:, e, lo : lo + n],
                        func=ACT.Tanh,
                        bias=bias_gate[:, 2 * a + e : 2 * a + e + 1],
                        scale=0.5,
                    )
            return gate

        def subtract_state(c, a, cand, engine=None):
            g_hx, u_hx = divmod(a, 2)
            for h in range(2):
                hx_t = hx_grouped[c, h][:].rearrange("p (g r t) -> p g t r", g=2, t=4)
                (engine or nc.vector).tensor_tensor(
                    out=cand[:, h], in0=cand[:, h], in1=hx_t[:, g_hx, 2 * u_hx : 2 * u_hx + 2, :], op=ALU.subtract
                )

        def add_rec(cand, rec):
            for h in range(2):
                nc.vector.tensor_tensor(out=cand[:, h], in0=cand[:, h], in1=rec[:, h], op=ALU.add)

        def multiply(cand, gate, blend, h):
            nc.vector.scalar_tensor_tensor(
                out=blend[:, h], in0=gate[:, h], scalar=1.0, in1=cand[:, h], op0=ALU.add, op1=ALU.mult
            )

        out_dram = out.rearrange("(p n) h -> p n h", n=ROWS)

        def transpose_back(blend, half):
            bank = psum.tile([P, 2, 2, P], F32, name="bank", tag="bank")
            for e in range(2):
                for n in range(2):
                    nc.tensor.transpose(bank[:, e, n, :], blend[:, half, e, P * n : P * (n + 1)], ident[:])
            return bank

        def state_bank(c, a, half):
            features = slice(2 * P * a, 2 * P * (a + 1))
            bank = psum.tile([P, 2, 2, P], F32, name="bank", tag="bank")
            nc.tensor.matmul(
                bank[:],
                lhsT=twice[:],
                rhs=hx_nat[c, half][:, :, features].rearrange("b n (p e) -> b e n p", e=2),
                start=True,
                stop=False,
            )
            return bank

        def add_transposed(bank, blend, half):
            for e in range(2):
                for n in range(2):
                    nc.tensor.matmul(
                        bank[:, e, n, :],
                        lhsT=blend[:, half, e, P * n : P * (n + 1)],
                        rhs=ident[:],
                        is_transpose=True,
                        start=False,
                        stop=e == 1 and n == 1,
                    )

        def finish_by_tiles(c, a, cand, gate):
            features = slice(2 * P * a, 2 * P * (a + 1))
            banks = []
            for n in range(CHUNK_ROWS):
                bank = psum.tile([P, 2, P], F32, name="bank", tag="bank")
                nc.tensor.matmul(
                    bank[:],
                    lhsT=twice[:],
                    rhs=hx_nat[c, n // HALF_ROWS][:, n % HALF_ROWS, features].rearrange("b (p e) -> b e p", e=2),
                    start=True,
                    stop=False,
                )
                banks.append(bank)
            blend = work.tile([P, 2, 2, HALF], F32, name="blend", bufs=3)
            for h, e, lo, n in last_pieces():
                nc.vector.scalar_tensor_tensor(
                    out=blend[:, h, e, lo : lo + n],
                    in0=gate[:, h, e, lo : lo + n],
                    scalar=1.0,
                    in1=cand[:, h, e, lo : lo + n],
                    op0=ALU.add,
                    op1=ALU.mult,
                )
            for n in range(CHUNK_ROWS):
                h, first = n // HALF_ROWS, P * (n % HALF_ROWS)
                for e in range(2):
                    nc.tensor.matmul(
                        banks[n][:, e, :],
                        lhsT=blend[:, h, e, first : first + P],
                        rhs=ident[:],
                        is_transpose=True,
                        start=False,
                        stop=e == 1,
                    )
                out_last = work.tile([P, 2 * P], F32, name="out_last", bufs=8)
                target = out_last[:].rearrange("b (p e) -> b p e", e=2)
                source = banks[n][:].rearrange("b e p -> b p e")
                if n % 2 == 0:
                    nc.scalar.mul(target, source, 0.5)
                else:
                    nc.vector.tensor_scalar_mul(out=target, in0=source, scalar1=0.5)
                nc.sync.dma_start(out=out_dram[:, CHUNK_ROWS * c + n, features], in_=out_last[:])

        def halve_and_store(c, a, half, bank, on_vector):
            features = slice(2 * P * a, 2 * P * (a + 1))
            first = CHUNK_ROWS * c + 2 * half
            for n in range(2):
                out_last = work.tile([P, 2 * P], F32, name="out_last", bufs=8)
                target = out_last[:].rearrange("b (p e) -> b p e", e=2)
                source = bank[:, :, n, :].rearrange("b e p -> b p e")
                if on_vector:
                    nc.vector.tensor_scalar_mul(out=target, in0=source, scalar1=0.5)
                else:
                    nc.scalar.mul(target, source, 0.5)
                nc.sync.dma_start(out=out_dram[:, first + n, features], in_=out_last[:])

        def add_state_and_store(c, a, half, bank, queue):
            features = slice(2 * P * a, 2 * P * (a + 1))
            first = CHUNK_ROWS * c + 2 * half
            out_rows = spare.pop(0)
            nc.vector.scalar_tensor_tensor(
                out=out_rows.rearrange("b n (p e) -> b n p e", e=2),
                in0=bank[:].rearrange("b e n p -> b n p e"),
                scalar=0.5,
                in1=hx_nat[c, half][:, :, features].rearrange("b n (p e) -> b n p e", e=2),
                op0=ALU.mult,
                op1=ALU.add,
            )
            queue.dma_start(out=out_dram[:, first : first + 2, features], in_=out_rows)

        raws = []

        def load_next():
            if len(raws) < len(units):
                raws.append(units[len(raws)][0]())

        for i in range(AHEAD):
            load_next()
            if 0 < i < 4:
                load_bias(2 * i - 2)
                load_bias(2 * i - 1)

        prepared = []

        def prepare_unit(vector_helps):
            i = len(prepared)
            prepared.append(i)
            fresh = units[i][1](raws[i], vector_helps)
            load_next()
            return fresh

        for i in range(HEAD):
            quantise(prepare_unit(i == 0))

        bank = psum.tile([P, 2, 2, P], F32, name="bank", tag="bank")
        nc.tensor.transpose(bank[:, 0, 0, :], bias_rows[:].bitcast(F32), ident[:])
        bias = keep.tile([P, 6, TILES], F32, name="bias")
        nc.vector.tensor_copy(
            out=bias[:].rearrange("p v j -> p (v j)"), in_=bank[:, 0, 0, 0 : 3 * TILES].bitcast(BF16)
        )
        bias_gate = keep.tile([P, TILES], F32, name="bias_gate")
        nc.gpsimd.tensor_tensor(out=bias_gate[:], in0=bias[:, 1, :], in1=bias[:, 2, :], op=ALU.add)
        bias_cand = keep.tile([P, TILES], F32, name="bias_cand")
        nc.gpsimd.tensor_tensor(out=bias_cand[:], in0=bias[:, 3, :], in1=bias[:, 4, :], op=ALU.add)
        nc.gpsimd.tensor_scalar(out=bias_gate[:], in0=bias_gate[:], scalar1=0.5, scalar2=None, op0=ALU.mult)

        fresh = []
        pairs = [(c, a) for c in range(CHUNKS) for a in range(PAIRS)]
        for (c, a), count in zip(pairs, FIRST_UNITS):
            for i in range(count):
                fresh += prepare_unit(i == 1 or (c, a) == (0, 1))
            quantise(fresh)
            fresh = []
            for args in first_layer_pair(c, a):
                fresh += interleave(*args)

        spare = []
        for name in ("ff1", "wff2"):
            block = keep.tile([P, 4, 2, 2 * P], F32, name=name + "_codes", align_bytes=256)
            spare += [block[:, i] for i in range(4)]
        for i in range(4):
            out_rows = work.tile([P, 2, 2 * P], F32, name="out_rows", bufs=4)
            spare.append(out_rows[:])

        blended = None
        returned = []
        pairs = [(c, a) for a in range(PAIRS) for c in range(CHUNKS)]
        cands = [input_product(*pairs[0])]
        for k, count in enumerate(SECOND_UNITS):
            c, a = pairs[k]
            last = k == len(pairs) - 1
            cand = cands[k]
            for back in returned:
                add_state_and_store(*back, nc.sync)
            quantise(fresh)
            rec = state_product(c, a)
            subtract_state(c, a, cand)
            add_rec(cand, rec)
            if last:
                gate = gate_product_by_halves(c, a)
                break
            gate = gate_product(c, a)
            fresh = []
            for i in range(count):
                fresh += prepare_unit(False)
            blend = work.tile([P, 2, 2, HALF], F32, name="blend", bufs=3)
            for h in range(2):
                multiply(cand, gate, blend, h)
            if blended is not None:
                returned = [(blended[0], blended[1], h, transpose_back(blended[2], h)) for h in range(2)]
            blended = (c, a, blend)
            cands.append(input_product(*pairs[k + 1]))
        banks = [state_bank(blended[0], blended[1], h) for h in range(2)]
        for h in range(2):
            add_transposed(banks[h], blended[2], h)
            halve_and_store(blended[0], blended[1], h, banks[h], False)
        finish_by_tiles(c, a, cand, gate)
